import numpy as np
import ml_dtypes


def mxq(x, axis, fmt="e4m3"):
    dtype, down = {"e4m3": (ml_dtypes.float8_e4m3fn, 7), "e5m2": (ml_dtypes.float8_e5m2, 14)}[fmt]
    v = np.moveaxis(np.asarray(x, np.float32).astype(ml_dtypes.bfloat16).astype(np.float64), axis, -1)
    blocks = v.reshape(v.shape[:-1] + (-1, 32))
    amax = np.abs(blocks).max(-1, keepdims=True)
    byte = np.maximum(np.where(amax > 0, np.frexp(amax)[1] - 1 + 127, 0) - down, 1)
    scale = np.exp2(byte - 127.0)
    codes = (blocks / scale).astype(np.float32).astype(dtype).astype(np.float64)
    return np.moveaxis((codes * scale).reshape(v.shape), -1, axis)


WIDE = False


def mx_kscale(k):
    if not WIDE:
        return np.ones(k)
    levels = np.array([20, -20, 10, -10, 0])
    a = np.random.permutation(np.resize(levels, k // 512 * 4)).reshape(k // 512, 4)
    idx = np.arange(k)
    return np.exp2(a[idx // 512, idx % 128 // 32])


BF16 = ml_dtypes.bfloat16


def bf(x):
    return np.asarray(x, np.float32).astype(BF16)


def f64(x):
    return np.asarray(x).astype(np.float64)


B, CIN, COUT, T, R, C = 2, 1024, 512, 8, 8, 8


def setup_inputs():
    u = mx_kscale(COUT)
    x = np.random.standard_normal((B, CIN, T, R, C))
    W = np.random.standard_normal((7 * COUT, CIN)) * 0.5 / np.sqrt(CIN) / np.tile(u, 7)[:, None]
    g = np.random.standard_normal((B, COUT, T, R, C)) * np.exp2(np.random.randint(-12, 1, (B, 1, T, R, C))) * 8.0 * u[None, :, None, None, None]
    return {"x": bf(x), "W": bf(W), "grad_out": bf(g)}


def _shift(a, axis, d):
    pads = [(0, 0)] * a.ndim
    idx = [slice(None)] * a.ndim
    if d > 0:
        pads[axis] = (1, 0)
        idx[axis] = slice(0, -1)
    else:
        pads[axis] = (0, 1)
        idx[axis] = slice(1, None)
    return np.pad(a, pads)[tuple(idx)]


def reference(x, W, grad_out):
    cout = W.shape[0] // 7
    cin = W.shape[1]
    gq = mxq(f64(grad_out), 1, "e5m2")
    Wq = mxq(f64(W).reshape(7, cout, cin), 1, "e4m3")
    gt = gq.transpose(0, 2, 3, 4, 1)
    Wm = Wq.transpose(1, 0, 2).reshape(cout, 7 * cin)
    z = gt @ Wm
    z = z.reshape(*z.shape[:4], 7, cin)
    out = z[..., 0, :]
    out = out + _shift(z[..., 1, :], 1, -1)
    out = out + _shift(z[..., 2, :], 1, +1)
    out = out + _shift(z[..., 3, :], 2, -1)
    out = out + _shift(z[..., 4, :], 2, +1)
    out = out + _shift(z[..., 5, :], 3, -1)
    out = out + _shift(z[..., 6, :], 3, +1)
    return np.transpose(out, (0, 4, 1, 2, 3))

@@ -1,0 +1,272 @@
+from contextlib import ExitStack
+
+import concourse.mybir as mybir
+
+F32 = mybir.dt.float32
+BF16 = mybir.dt.bfloat16
+U32 = mybir.dt.uint32
+I32 = mybir.dt.int32
+U8 = mybir.dt.uint8
+E4M3X4 = mybir.dt.float8_e4m3fn_x4
+E5M2X4 = mybir.dt.float8_e5m2_x4
+
+P = 128
+PACK = 4
+NB = 2
+CIN = 1024
+COUT = 512
+VOX = 512
+NDIR = 7
+HALF = 512
+PAD = 64
+
+FLOPS = 2 * NB * VOX * COUT * NDIR * CIN
+BYTES = NDIR * COUT * CIN * 2 + NB * COUT * VOX * 2 + NB * CIN * VOX * 4
+
+MANUAL = False
+S_COLS = (384, 192)
+
+
+def tile_stackeddirectionalconv3d_t_kernel(tc, x, W, grad_out, out):
+    nc = tc.nc
+    w_view = W.rearrange("(k p j) i -> k p j i", k=NDIR, j=PACK)
+    g_view = grad_out.rearrange("b (p j) t r c -> b p j (t r c)", j=PACK)
+    o_view = out.rearrange("b (m p) t r c -> b m p (t r c)", p=P)
+
+    with ExitStack() as ctx:
+        keep = ctx.enter_context(tc.tile_pool(name="keep", bufs=1))
+        stage = ctx.enter_context(tc.tile_pool(name="stage", bufs=4))
+        outp = ctx.enter_context(tc.tile_pool(name="outp", bufs=6))
+        psum = ctx.enter_context(tc.psum_pool(name="psum", bufs=1))
+        if MANUAL:
+            ctx.enter_context(tc.manual_schedule())
+
+        g_raw = keep.tile([P, NB, PACK, VOX], BF16, name="g_raw")
+        g_grp = keep.tile([P, NB, VOX, PACK], BF16, name="g_grp", align_bytes=64)
+        g_sh = [
+            keep.tile([P, NB, VOX, PACK], BF16, name="g_sh%d" % d, align_bytes=64)
+            for d in range(2)
+        ]
+        base_c = keep.tile([P, NB, VOX + 2 * PAD], U32, name="base_c", align_bytes=64)
+        base_s = keep.tile([P, NB, VOX + 2 * PAD], U8, name="base_s", align_bytes=64)
+        dir_c = [
+            keep.tile([P, NB, VOX], U32, name="dir_c%d" % d, align_bytes=64)
+            for d in range(4)
+        ]
+        dir_s = [
+            keep.tile([P, NB, VOX], U8, name="dir_s%d" % d, align_bytes=64)
+            for d in range(4)
+        ]
+        w_raw = {}
+        w_c = {}
+        w_s = {}
+        for h in range(2):
+            for k in range(NDIR):
+                w_raw[(k, h)] = keep.tile([P, PACK, HALF], BF16, name="w_raw%d_%d" % (k, h))
+                w_c[(k, h)] = keep.tile([P, HALF], U32, name="w_c%d_%d" % (k, h), align_bytes=64)
+                w_s[(k, h)] = keep.tile([P, HALF], U8, name="w_s%d_%d" % (k, h), align_bytes=64)
+        w_grp = {}
+
+        base_c32 = base_c[:].bitcast(I32)
+        base_s32 = base_s[:].bitcast(I32)
+        data_c32 = base_c32[:, :, PAD : PAD + VOX].rearrange("p b (t q) -> p b t q", q=64)
+        data_s32 = base_s32[:, :, PAD // 4 : (PAD + VOX) // 4].rearrange("p b (t q) -> p b t q", q=16)
+        dir_c32 = [dir_c[d][:].bitcast(I32).rearrange("p b (t q) -> p b t q", q=64) for d in range(2)]
+        dir_s32 = [dir_s[d][:].bitcast(I32).rearrange("p b (t q) -> p b t q", q=16) for d in range(2)]
+        grp_rows = g_grp[:].rearrange("p b (a c) j -> p (b a) (c j)", c=8)
+        sh_rows = [g_sh[d][:].rearrange("p b (a c) j -> p (b a) (c j)", c=8) for d in range(2)]
+
+        nc.vector.memset(base_s32, 0)
+        nc.vector.memset(base_c32[:, :, 0:PAD], 0)
+        nc.vector.memset(base_c32[:, :, PAD + VOX : PAD + VOX + PAD], 0)
+        nc.vector.memset(dir_c32[0][:, :, :, 56:64], 0)
+        nc.vector.memset(dir_c32[1][:, :, :, 0:8], 0)
+        nc.vector.memset(dir_s32[0][:, :, :, 14:16], 0)
+        nc.vector.memset(dir_s32[1][:, :, :, 0:2], 0)
+        nc.vector.memset(sh_rows[0][:, :, 28:32], 0.0)
+        nc.vector.memset(sh_rows[1][:, :, 0:4], 0.0)
+
+        def load_w(k, h):
+            nc.sync.dma_start(out=w_raw[(k, h)][:], in_=w_view[k][:, :, h * HALF : (h + 1) * HALF])
+
+        def load_g(b):
+            nc.sync.dma_start(out=g_raw[:, b], in_=g_view[b])
+
+        load_g(0)
+        load_w(0, 0)
+        load_g(1)
+        for k in range(1, NDIR):
+            load_w(k, 0)
+        for k in range(NDIR):
+            load_w(k, 1)
+
+        def regroup(engine_copy, dst, src):
+            engine_copy(
+                out=dst.rearrange("p (c i) t -> p c t i", i=4),
+                in_=src.rearrange("p t (c i) -> p c t i", i=4),
+            )
+
+        def regroup_g(b):
+            regroup(nc.vector.tensor_copy, g_grp[:, b], g_raw[:, b])
+
+        def quant_g(b):
+            nc.vector.quantize_mx(
+                out=base_c[:, b, PAD : PAD + VOX].bitcast(E5M2X4),
+                scales=base_s[:, b, PAD : PAD + VOX],
+                in_=g_grp[:, b].rearrange("p w j -> p (w j)"),
+            )
+
+        def moves_r(d):
+            if d == 0:
+                nc.vector.tensor_copy(out=dir_c32[0][:, :, :, 0:56], in_=data_c32[:, :, :, 8:64])
+                nc.vector.tensor_copy(out=dir_s32[0][:, :, :, 0:14], in_=data_s32[:, :, :, 2:16])
+            else:
+                nc.vector.tensor_copy(out=dir_c32[1][:, :, :, 8:64], in_=data_c32[:, :, :, 0:56])
+                nc.vector.tensor_copy(out=dir_s32[1][:, :, :, 2:16], in_=data_s32[:, :, :, 0:14])
+
+        def shift_c(d):
+            if d == 0:
+                nc.vector.tensor_copy(out=sh_rows[0][:, :, 0:28], in_=grp_rows[:, :, 4:32])
+            else:
+                nc.vector.tensor_copy(out=sh_rows[1][:, :, 4:32], in_=grp_rows[:, :, 0:28])
+
+        def quant_c(d):
+            nc.vector.quantize_mx(
+                out=dir_c[2 + d][:].rearrange("p b v -> p (b v)").bitcast(E5M2X4),
+                scales=dir_s[2 + d][:].rearrange("p b v -> p (b v)"),
+                in_=g_sh[d][:].rearrange("p b w j -> p (b w j)"),
+            )
+
+        def regroup_w(k, h):
+            grp = stage.tile([P, HALF, PACK], BF16, tag="w_grp", name="w_grp%d_%d" % (k, h), align_bytes=64)
+            w_grp[(k, h)] = grp
+            sc = S_COLS[h]
+            regroup(nc.scalar.copy, grp[:, 0:sc, :], w_raw[(k, h)][:, :, 0:sc])
+            regroup(nc.vector.tensor_copy, grp[:, sc:HALF, :], w_raw[(k, h)][:, :, sc:HALF])
+
+        def quant_w(k, h):
+            nc.vector.quantize_mx(
+                out=w_c[(k, h)][:].bitcast(E4M3X4),
+                scales=w_s[(k, h)][:],
+                in_=w_grp[(k, h)][:].rearrange("p w j -> p (w j)"),
+            )
+
+        def moving(k, b):
+            if k == 0:
+                return base_c[:, b, PAD : PAD + VOX], base_s[:, b, PAD : PAD + VOX]
+            if k == 1:
+                return base_c[:, b, 2 * PAD : 2 * PAD + VOX], base_s[:, b, 2 * PAD : 2 * PAD + VOX]
+            if k == 2:
+                return base_c[:, b, 0:VOX], base_s[:, b, 0:VOX]
+            return dir_c[k - 3][:, b, :], dir_s[k - 3][:, b, :]
+
+        acc = {}
+
+        def mx_pass(k, m, b, bank):
+            if k == 0:
+                acc[(m, b)] = psum.tile([P, VOX], F32, tag="bank%d" % bank, name="acc%d_%d" % (m, b))
+            h = m // 4
+            cols = slice((m % 4) * P, (m % 4 + 1) * P)
+            codes, scales = moving(k, b)
+            nc.tensor.matmul_mx(
+                out=acc[(m, b)][:],
+                lhsT=w_c[(k, h)][:, cols].bitcast(E4M3X4),
+                lhsT_scale=w_s[(k, h)][:, cols],
+                rhs=codes.bitcast(E5M2X4),
+                rhs_scale=scales,
+                start=(k == 0),
+                stop=(k == NDIR - 1),
+            )
+
+        def evac(m, b, on_vector):
+            res = outp.tile([P, VOX], F32, tag="res", name="res%d_%d" % (m, b))
+            if on_vector:
+                nc.vector.tensor_copy(out=res[:], in_=acc[(m, b)][:])
+            else:
+                nc.scalar.copy(out=res[:], in_=acc[(m, b)][:])
+            nc.sync.dma_start(out=o_view[b, m], in_=res[:])
+
+        def round1(k, bs):
+            for b in bs:
+                for m in range(4):
+                    mx_pass(k, m, b, 2 * m + b)
+
+        def round_a(k):
+            for m in (4, 5):
+                for b in range(NB):
+                    mx_pass(k, m, b, 2 * (m - 4) + b)
+
+        regroup_g(0)
+        regroup_w(0, 0)
+        quant_g(0)
+        regroup_g(1)
+        quant_w(0, 0)
+        round1(0, (0,))
+        regroup_w(1, 0)
+        quant_g(1)
+        round1(0, (1,))
+        regroup_w(2, 0)
+        quant_w(1, 0)
+        round1(1, (0, 1))
+        moves_r(0)
+        regroup_w(3, 0)
+        quant_w(2, 0)
+        round1(2, (0, 1))
+        moves_r(1)
+        regroup_w(4, 0)
+        quant_w(3, 0)
+        round1(3, (0, 1))
+        shift_c(0)
+        regroup_w(5, 0)
+        quant_w(4, 0)
+        round1(4, (0, 1))
+        quant_c(0)
+        shift_c(1)
+        regroup_w(6, 0)
+        quant_w(5, 0)
+        round1(5, (0, 1))
+        quant_c(1)
+        regroup_w(0, 1)
+        quant_w(6, 0)
+        for m in range(4):
+            for b in range(NB):
+                mx_pass(6, m, b, 2 * m + b)
+
+        regroup_w(1, 1)
+        quant_w(0, 1)
+        regroup_w(2, 1)
+        quant_w(1, 1)
+        regroup_w(3, 1)
+        quant_w(2, 1)
+        for m in (0, 1):
+            for b in range(NB):
+                evac(m, b, False)
+        round_a(0)
+        round_a(1)
+        round_a(2)
+        regroup_w(4, 1)
+        quant_w(3, 1)
+        round_a(3)
+        regroup_w(5, 1)
+        quant_w(4, 1)
+        round_a(4)
+        regroup_w(6, 1)
+        quant_w(5, 1)
+        round_a(5)
+        for m in (2, 3):
+            for b in range(NB):
+                evac(m, b, False)
+        quant_w(6, 1)
+        round_a(6)
+        n = 0
+        for m in (6, 7):
+            for b in range(NB):
+                for k in range(NDIR):
+                    mx_pass(k, m, b, 4 + 2 * (m - 6) + b)
+                if n == 0:
+                    evac(4, 0, False)
+                    evac(4, 1, True)
+                    evac(5, 0, False)
+                    evac(5, 1, True)
+                n += 1
+                evac(m, b, n % 2 == 0)

@@ -23,8 +23,7 @@ PAD = 64
 FLOPS = 2 * NB * VOX * COUT * NDIR * CIN
 BYTES = NDIR * COUT * CIN * 2 + NB * COUT * VOX * 2 + NB * CIN * VOX * 4
 
-MANUAL = False
-S_COLS = (384, 192)
+MANUAL = True
 
 
 def tile_stackeddirectionalconv3d_t_kernel(tc, x, W, grad_out, out):
@@ -66,6 +65,7 @@ def tile_stackeddirectionalconv3d_t_kernel(tc, x, W, grad_out, out):
                 w_c[(k, h)] = keep.tile([P, HALF], U32, name="w_c%d_%d" % (k, h), align_bytes=64)
                 w_s[(k, h)] = keep.tile([P, HALF], U8, name="w_s%d_%d" % (k, h), align_bytes=64)
         w_grp = {}
+        acc = {}
 
         base_c32 = base_c[:].bitcast(I32)
         base_s32 = base_s[:].bitcast(I32)
@@ -86,37 +86,32 @@ def tile_stackeddirectionalconv3d_t_kernel(tc, x, W, grad_out, out):
         nc.vector.memset(sh_rows[0][:, :, 28:32], 0.0)
         nc.vector.memset(sh_rows[1][:, :, 0:4], 0.0)
 
-        def load_w(k, h):
-            nc.sync.dma_start(out=w_raw[(k, h)][:], in_=w_view[k][:, :, h * HALF : (h + 1) * HALF])
+        def lw(k, h, c0, c1):
+            nc.sync.dma_start(
+                out=w_raw[(k, h)][:, :, c0:c1], in_=w_view[k][:, :, h * HALF + c0 : h * HALF + c1]
+            )
 
-        def load_g(b):
-            nc.sync.dma_start(out=g_raw[:, b], in_=g_view[b])
+        def lg(b, v0, v1):
+            nc.sync.dma_start(out=g_raw[:, b, :, v0:v1], in_=g_view[b][:, :, v0:v1])
 
-        load_g(0)
-        load_w(0, 0)
-        load_g(1)
-        for k in range(1, NDIR):
-            load_w(k, 0)
-        for k in range(NDIR):
-            load_w(k, 1)
-
-        def regroup(engine_copy, dst, src):
-            engine_copy(
+        def regroup(on_vector, dst, src):
+            copy = nc.vector.tensor_copy if on_vector else nc.scalar.copy
+            copy(
                 out=dst.rearrange("p (c i) t -> p c t i", i=4),
                 in_=src.rearrange("p t (c i) -> p c t i", i=4),
             )
 
-        def regroup_g(b):
-            regroup(nc.vector.tensor_copy, g_grp[:, b], g_raw[:, b])
+        def rg(b, v0, v1, on_vector):
+            regroup(on_vector, g_grp[:, b, v0:v1, :], g_raw[:, b, :, v0:v1])
 
-        def quant_g(b):
+        def qg(b, v0, v1):
             nc.vector.quantize_mx(
-                out=base_c[:, b, PAD : PAD + VOX].bitcast(E5M2X4),
-                scales=base_s[:, b, PAD : PAD + VOX],
-                in_=g_grp[:, b].rearrange("p w j -> p (w j)"),
+                out=base_c[:, b, PAD + v0 : PAD + v1].bitcast(E5M2X4),
+                scales=base_s[:, b, PAD + v0 : PAD + v1],
+                in_=g_grp[:, b, v0:v1, :].rearrange("p w j -> p (w j)"),
             )
 
-        def moves_r(d):
+        def mr(d):
             if d == 0:
                 nc.vector.tensor_copy(out=dir_c32[0][:, :, :, 0:56], in_=data_c32[:, :, :, 8:64])
                 nc.vector.tensor_copy(out=dir_s32[0][:, :, :, 0:14], in_=data_s32[:, :, :, 2:16])
@@ -124,31 +119,31 @@ def tile_stackeddirectionalconv3d_t_kernel(tc, x, W, grad_out, out):
                 nc.vector.tensor_copy(out=dir_c32[1][:, :, :, 8:64], in_=data_c32[:, :, :, 0:56])
                 nc.vector.tensor_copy(out=dir_s32[1][:, :, :, 2:16], in_=data_s32[:, :, :, 0:14])
 
-        def shift_c(d):
+        def sc(d):
             if d == 0:
                 nc.vector.tensor_copy(out=sh_rows[0][:, :, 0:28], in_=grp_rows[:, :, 4:32])
             else:
                 nc.vector.tensor_copy(out=sh_rows[1][:, :, 4:32], in_=grp_rows[:, :, 0:28])
 
-        def quant_c(d):
+        def qc(d):
             nc.vector.quantize_mx(
                 out=dir_c[2 + d][:].rearrange("p b v -> p (b v)").bitcast(E5M2X4),
                 scales=dir_s[2 + d][:].rearrange("p b v -> p (b v)"),
                 in_=g_sh[d][:].rearrange("p b w j -> p (b w j)"),
             )
 
-        def regroup_w(k, h):
-            grp = stage.tile([P, HALF, PACK], BF16, tag="w_grp", name="w_grp%d_%d" % (k, h), align_bytes=64)
-            w_grp[(k, h)] = grp
-            sc = S_COLS[h]
-            regroup(nc.scalar.copy, grp[:, 0:sc, :], w_raw[(k, h)][:, :, 0:sc])
-            regroup(nc.vector.tensor_copy, grp[:, sc:HALF, :], w_raw[(k, h)][:, :, sc:HALF])
+        def rw(k, h, c0, c1, on_vector):
+            if (k, h) not in w_grp:
+                w_grp[(k, h)] = stage.tile(
+                    [P, HALF, PACK], BF16, tag="w_grp", name="w_grp%d_%d" % (k, h), align_bytes=64
+                )
+            regroup(on_vector, w_grp[(k, h)][:, c0:c1, :], w_raw[(k, h)][:, :, c0:c1])
 
-        def quant_w(k, h):
+        def qw(k, h, c0, c1):
             nc.vector.quantize_mx(
-                out=w_c[(k, h)][:].bitcast(E4M3X4),
-                scales=w_s[(k, h)][:],
-                in_=w_grp[(k, h)][:].rearrange("p w j -> p (w j)"),
+                out=w_c[(k, h)][:, c0:c1].bitcast(E4M3X4),
+                scales=w_s[(k, h)][:, c0:c1],
+                in_=w_grp[(k, h)][:, c0:c1, :].rearrange("p w j -> p (w j)"),
             )
 
         def moving(k, b):
@@ -160,9 +155,7 @@ def tile_stackeddirectionalconv3d_t_kernel(tc, x, W, grad_out, out):
                 return base_c[:, b, 0:VOX], base_s[:, b, 0:VOX]
             return dir_c[k - 3][:, b, :], dir_s[k - 3][:, b, :]
 
-        acc = {}
-
-        def mx_pass(k, m, b, bank):
+        def mx(k, m, b, bank):
             if k == 0:
                 acc[(m, b)] = psum.tile([P, VOX], F32, tag="bank%d" % bank, name="acc%d_%d" % (m, b))
             h = m // 4
@@ -178,7 +171,7 @@ def tile_stackeddirectionalconv3d_t_kernel(tc, x, W, grad_out, out):
                 stop=(k == NDIR - 1),
             )
 
-        def evac(m, b, on_vector):
+        def ev(m, b, on_vector):
             res = outp.tile([P, VOX], F32, tag="res", name="res%d_%d" % (m, b))
             if on_vector:
                 nc.vector.tensor_copy(out=res[:], in_=acc[(m, b)][:])
@@ -186,87 +179,201 @@ def tile_stackeddirectionalconv3d_t_kernel(tc, x, W, grad_out, out):
                 nc.scalar.copy(out=res[:], in_=acc[(m, b)][:])
             nc.sync.dma_start(out=o_view[b, m], in_=res[:])
 
-        def round1(k, bs):
-            for b in bs:
-                for m in range(4):
-                    mx_pass(k, m, b, 2 * m + b)
-
-        def round_a(k):
-            for m in (4, 5):
-                for b in range(NB):
-                    mx_pass(k, m, b, 2 * (m - 4) + b)
-
-        regroup_g(0)
-        regroup_w(0, 0)
-        quant_g(0)
-        regroup_g(1)
-        quant_w(0, 0)
-        round1(0, (0,))
-        regroup_w(1, 0)
-        quant_g(1)
-        round1(0, (1,))
-        regroup_w(2, 0)
-        quant_w(1, 0)
-        round1(1, (0, 1))
-        moves_r(0)
-        regroup_w(3, 0)
-        quant_w(2, 0)
-        round1(2, (0, 1))
-        moves_r(1)
-        regroup_w(4, 0)
-        quant_w(3, 0)
-        round1(3, (0, 1))
-        shift_c(0)
-        regroup_w(5, 0)
-        quant_w(4, 0)
-        round1(4, (0, 1))
-        quant_c(0)
-        shift_c(1)
-        regroup_w(6, 0)
-        quant_w(5, 0)
-        round1(5, (0, 1))
-        quant_c(1)
-        regroup_w(0, 1)
-        quant_w(6, 0)
-        for m in range(4):
-            for b in range(NB):
-                mx_pass(6, m, b, 2 * m + b)
-
-        regroup_w(1, 1)
-        quant_w(0, 1)
-        regroup_w(2, 1)
-        quant_w(1, 1)
-        regroup_w(3, 1)
-        quant_w(2, 1)
-        for m in (0, 1):
-            for b in range(NB):
-                evac(m, b, False)
-        round_a(0)
-        round_a(1)
-        round_a(2)
-        regroup_w(4, 1)
-        quant_w(3, 1)
-        round_a(3)
-        regroup_w(5, 1)
-        quant_w(4, 1)
-        round_a(4)
-        regroup_w(6, 1)
-        quant_w(5, 1)
-        round_a(5)
-        for m in (2, 3):
-            for b in range(NB):
-                evac(m, b, False)
-        quant_w(6, 1)
-        round_a(6)
-        n = 0
-        for m in (6, 7):
-            for b in range(NB):
-                for k in range(NDIR):
-                    mx_pass(k, m, b, 4 + 2 * (m - 6) + b)
-                if n == 0:
-                    evac(4, 0, False)
-                    evac(4, 1, True)
-                    evac(5, 0, False)
-                    evac(5, 1, True)
-                n += 1
-                evac(m, b, n % 2 == 0)
+        lg(0, 0, 256)
+        lg(0, 256, 512)
+        lw(0, 0, 0, 128)
+        lw(0, 0, 128, 512)
+        lg(1, 0, 256)
+        lg(1, 256, 512)
+        lw(1, 0, 0, 512)
+        lw(2, 0, 0, 512)
+        lw(3, 0, 0, 512)
+        lw(4, 0, 0, 512)
+        lw(5, 0, 0, 512)
+        lw(6, 0, 0, 512)
+        lw(0, 1, 0, 512)
+        lw(1, 1, 0, 512)
+        lw(2, 1, 0, 512)
+        lw(3, 1, 0, 512)
+        lw(4, 1, 0, 512)
+        lw(5, 1, 0, 512)
+        lw(6, 1, 0, 512)
+        rg(0, 0, 256, True)
+        rw(0, 0, 0, 128, False)
+        rg(0, 256, 512, True)
+        rw(0, 0, 128, 256, False)
+        qg(0, 0, 256)
+        qg(0, 256, 512)
+        qw(0, 0, 0, 128)
+        rw(0, 0, 256, 384, False)
+        rg(1, 0, 256, True)
+        qw(0, 0, 128, 256)
+        rw(0, 0, 384, 512, False)
+        rg(1, 256, 512, True)
+        qw(0, 0, 256, 384)
+        qg(1, 0, 256)
+        qg(1, 256, 512)
+        qw(0, 0, 384, 512)
+        mx(0, 0, 0, 0)
+        mx(0, 1, 0, 2)
+        mx(0, 2, 0, 4)
+        mx(0, 0, 1, 1)
+        mx(0, 1, 1, 3)
+        mx(0, 2, 1, 5)
+        mx(0, 3, 0, 6)
+        mx(0, 3, 1, 7)
+        rw(1, 0, 0, 256, False)
+        rw(1, 0, 256, 512, True)
+        rw(2, 0, 0, 384, False)
+        qw(1, 0, 0, 256)
+        qw(1, 0, 256, 512)
+        mx(1, 0, 0, 0)
+        mx(1, 0, 1, 1)
+        mx(1, 1, 0, 2)
+        mx(1, 1, 1, 3)
+        mx(1, 2, 0, 4)
+        mx(1, 2, 1, 5)
+        mx(1, 3, 0, 6)
+        mx(1, 3, 1, 7)
+        rw(2, 0, 384, 512, True)
+        mr(0)
+        rw(3, 0, 0, 512, False)
+        qw(2, 0, 0, 512)
+        mx(2, 0, 0, 0)
+        mx(2, 0, 1, 1)
+        mx(2, 1, 0, 2)
+        mx(2, 1, 1, 3)
+        mx(2, 2, 0, 4)
+        mx(2, 2, 1, 5)
+        mx(2, 3, 0, 6)
+        mx(2, 3, 1, 7)
+        mr(1)
+        rw(4, 0, 0, 512, False)
+        sc(0)
+        qw(3, 0, 0, 512)
+        mx(3, 0, 0, 0)
+        mx(3, 0, 1, 1)
+        mx(3, 1, 0, 2)
+        mx(3, 1, 1, 3)
+        mx(3, 2, 0, 4)
+        mx(3, 2, 1, 5)
+        mx(3, 3, 0, 6)
+        mx(3, 3, 1, 7)
+        qc(0)
+        rw(5, 0, 0, 512, False)
+        qw(4, 0, 0, 512)
+        mx(4, 0, 0, 0)
+        mx(4, 0, 1, 1)
+        mx(4, 1, 0, 2)
+        mx(4, 1, 1, 3)
+        mx(4, 2, 0, 4)
+        mx(4, 2, 1, 5)
+        mx(4, 3, 0, 6)
+        mx(4, 3, 1, 7)
+        sc(1)
+        rw(6, 0, 0, 512, False)
+        qw(5, 0, 0, 512)
+        mx(5, 0, 0, 0)
+        mx(5, 0, 1, 1)
+        mx(5, 1, 0, 2)
+        mx(5, 1, 1, 3)
+        mx(5, 2, 0, 4)
+        mx(5, 2, 1, 5)
+        mx(5, 3, 0, 6)
+        mx(5, 3, 1, 7)
+        qc(1)
+        rw(0, 1, 0, 512, False)
+        rw(1, 1, 0, 512, True)
+        qw(6, 0, 0, 512)
+        mx(6, 0, 0, 0)
+        mx(6, 0, 1, 1)
+        mx(6, 1, 0, 2)
+        mx(6, 1, 1, 3)
+        mx(6, 2, 0, 4)
+        mx(6, 2, 1, 5)
+        mx(6, 3, 0, 6)
+        mx(6, 3, 1, 7)
+        qw(0, 1, 0, 512)
+        rw(2, 1, 0, 512, True)
+        qw(1, 1, 0, 512)
+        ev(0, 0, False)
+        ev(0, 1, False)
+        ev(1, 0, False)
+        ev(1, 1, False)
+        ev(2, 0, False)
+        ev(2, 1, False)
+        mx(0, 4, 0, 0)
+        mx(0, 4, 1, 1)
+        mx(0, 5, 0, 2)
+        mx(0, 5, 1, 3)
+        mx(0, 6, 0, 4)
+        mx(0, 6, 1, 5)
+        ev(3, 0, False)
+        ev(3, 1, False)
+        mx(1, 4, 0, 0)
+        mx(1, 4, 1, 1)
+        mx(1, 5, 0, 2)
+        mx(1, 5, 1, 3)
+        mx(1, 6, 0, 4)
+        mx(1, 6, 1, 5)
+        rw(3, 1, 0, 512, True)
+        qw(2, 1, 0, 512)
+        mx(2, 4, 0, 0)
+        mx(2, 4, 1, 1)
+        mx(2, 5, 0, 2)
+        mx(2, 5, 1, 3)
+        mx(2, 6, 0, 4)
+        mx(2, 6, 1, 5)
+        rw(4, 1, 0, 512, True)
+        qw(3, 1, 0, 512)
+        mx(3, 4, 0, 0)
+        mx(3, 4, 1, 1)
+        mx(3, 5, 0, 2)
+        mx(3, 5, 1, 3)
+        mx(3, 6, 0, 4)
+        mx(3, 6, 1, 5)
+        rw(5, 1, 0, 512, True)
+        qw(4, 1, 0, 512)
+        mx(4, 4, 0, 0)
+        mx(4, 4, 1, 1)
+        mx(4, 5, 0, 2)
+        mx(4, 5, 1, 3)
+        mx(4, 6, 0, 4)
+        mx(4, 6, 1, 5)
+        rw(6, 1, 0, 512, True)
+        qw(5, 1, 0, 512)
+        mx(5, 4, 0, 0)
+        mx(5, 4, 1, 1)
+        mx(5, 5, 0, 2)
+        mx(5, 5, 1, 3)
+        mx(5, 6, 0, 4)
+        mx(5, 6, 1, 5)
+        qw(6, 1, 0, 512)
+        mx(6, 4, 0, 0)
+        mx(6, 4, 1, 1)
+        mx(6, 5, 0, 2)
+        mx(6, 5, 1, 3)
+        mx(6, 6, 0, 4)
+        mx(6, 6, 1, 5)
+        mx(0, 7, 0, 6)
+        mx(1, 7, 0, 6)
+        mx(2, 7, 0, 6)
+        mx(3, 7, 0, 6)
+        mx(4, 7, 0, 6)
+        mx(5, 7, 0, 6)
+        mx(6, 7, 0, 6)
+        ev(4, 0, False)
+        ev(4, 1, True)
+        ev(5, 0, False)
+        ev(5, 1, True)
+        ev(6, 0, False)
+        ev(6, 1, True)
+        ev(7, 0, True)
+        mx(0, 7, 1, 7)
+        mx(1, 7, 1, 7)
+        mx(2, 7, 1, 7)
+        mx(3, 7, 1, 7)
+        mx(4, 7, 1, 7)
+        mx(5, 7, 1, 7)
+        mx(6, 7, 1, 7)
+        ev(7, 1, False)

@@ -19,6 +19,8 @@ VOX = 512
 NDIR = 7
 HALF = 512
 PAD = 64
+SPLANE = 768
+WOFF = 48
 
 FLOPS = 2 * NB * VOX * COUT * NDIR * CIN
 BYTES = NDIR * COUT * CIN * 2 + NB * COUT * VOX * 2 + NB * CIN * VOX * 4
@@ -46,14 +48,14 @@ def tile_stackeddirectionalconv3d_t_kernel(tc, x, W, grad_out, out):
             keep.tile([P, NB, VOX, PACK], BF16, name="g_sh%d" % d, align_bytes=64)
             for d in range(2)
         ]
-        base_c = keep.tile([P, NB, VOX + 2 * PAD], U32, name="base_c", align_bytes=64)
-        base_s = keep.tile([P, NB, VOX + 2 * PAD], U8, name="base_s", align_bytes=64)
+        base_c = keep.tile([P, NB, VOX + 2 * PAD], U32, name="base_c", align_bytes=256)
+        base_s = keep.tile([P, NB, SPLANE], U8, name="base_s", align_bytes=256)
         dir_c = [
-            keep.tile([P, NB, VOX], U32, name="dir_c%d" % d, align_bytes=64)
+            keep.tile([P, NB, VOX], U32, name="dir_c%d" % d, align_bytes=256)
             for d in range(4)
         ]
         dir_s = [
-            keep.tile([P, NB, VOX], U8, name="dir_s%d" % d, align_bytes=64)
+            keep.tile([P, NB, VOX], U8, name="dir_s%d" % d, align_bytes=256)
             for d in range(4)
         ]
         w_raw = {}
@@ -62,8 +64,8 @@ def tile_stackeddirectionalconv3d_t_kernel(tc, x, W, grad_out, out):
         for h in range(2):
             for k in range(NDIR):
                 w_raw[(k, h)] = keep.tile([P, PACK, HALF], BF16, name="w_raw%d_%d" % (k, h))
-                w_c[(k, h)] = keep.tile([P, HALF], U32, name="w_c%d_%d" % (k, h), align_bytes=64)
-                w_s[(k, h)] = keep.tile([P, HALF], U8, name="w_s%d_%d" % (k, h), align_bytes=64)
+                w_c[(k, h)] = keep.tile([P, WOFF + HALF], U32, name="w_c%d_%d" % (k, h), align_bytes=256)
+                w_s[(k, h)] = keep.tile([P, HALF], U8, name="w_s%d_%d" % (k, h), align_bytes=256)
         w_grp = {}
         acc = {}
 
@@ -141,7 +143,7 @@ def tile_stackeddirectionalconv3d_t_kernel(tc, x, W, grad_out, out):
 
         def qw(k, h, c0, c1):
             nc.vector.quantize_mx(
-                out=w_c[(k, h)][:, c0:c1].bitcast(E4M3X4),
+                out=w_c[(k, h)][:, WOFF + c0 : WOFF + c1].bitcast(E4M3X4),
                 scales=w_s[(k, h)][:, c0:c1],
                 in_=w_grp[(k, h)][:, c0:c1, :].rearrange("p w j -> p (w j)"),
             )
@@ -163,7 +165,7 @@ def tile_stackeddirectionalconv3d_t_kernel(tc, x, W, grad_out, out):
             codes, scales = moving(k, b)
             nc.tensor.matmul_mx(
                 out=acc[(m, b)][:],
-                lhsT=w_c[(k, h)][:, cols].bitcast(E4M3X4),
+                lhsT=w_c[(k, h)][:, WOFF + (m % 4) * P : WOFF + (m % 4 + 1) * P].bitcast(E4M3X4),
                 lhsT_scale=w_s[(k, h)][:, cols],
                 rhs=codes.bitcast(E5M2X4),
                 rhs_scale=scales,

@@ -181,12 +181,9 @@ def tile_stackeddirectionalconv3d_t_kernel(tc, x, W, grad_out, out):
                 nc.scalar.copy(out=res[:], in_=acc[(m, b)][:])
             nc.sync.dma_start(out=o_view[b, m], in_=res[:])
 
-        lg(0, 0, 256)
-        lg(0, 256, 512)
-        lw(0, 0, 0, 128)
-        lw(0, 0, 128, 512)
-        lg(1, 0, 256)
-        lg(1, 256, 512)
+        lg(0, 0, 512)
+        lw(0, 0, 0, 512)
+        lg(1, 0, 512)
         lw(1, 0, 0, 512)
         lw(2, 0, 0, 512)
         lw(3, 0, 0, 512)
@@ -216,6 +213,14 @@ def tile_stackeddirectionalconv3d_t_kernel(tc, x, W, grad_out, out):
         qg(1, 0, 256)
         qg(1, 256, 512)
         qw(0, 0, 384, 512)
+        rw(1, 0, 0, 256, False)
+        rw(1, 0, 256, 512, True)
+        rw(2, 0, 0, 384, False)
+        qw(1, 0, 0, 256)
+        qw(1, 0, 256, 512)
+        rw(2, 0, 384, 512, True)
+        mr(0)
+        qw(2, 0, 0, 512)
         mx(0, 0, 0, 0)
         mx(0, 1, 0, 2)
         mx(0, 2, 0, 4)
@@ -224,11 +229,6 @@ def tile_stackeddirectionalconv3d_t_kernel(tc, x, W, grad_out, out):
         mx(0, 2, 1, 5)
         mx(0, 3, 0, 6)
         mx(0, 3, 1, 7)
-        rw(1, 0, 0, 256, False)
-        rw(1, 0, 256, 512, True)
-        rw(2, 0, 0, 384, False)
-        qw(1, 0, 0, 256)
-        qw(1, 0, 256, 512)
         mx(1, 0, 0, 0)
         mx(1, 0, 1, 1)
         mx(1, 1, 0, 2)
@@ -237,10 +237,6 @@ def tile_stackeddirectionalconv3d_t_kernel(tc, x, W, grad_out, out):
         mx(1, 2, 1, 5)
         mx(1, 3, 0, 6)
         mx(1, 3, 1, 7)
-        rw(2, 0, 384, 512, True)
-        mr(0)
-        rw(3, 0, 0, 512, False)
-        qw(2, 0, 0, 512)
         mx(2, 0, 0, 0)
         mx(2, 0, 1, 1)
         mx(2, 1, 0, 2)
@@ -249,9 +245,9 @@ def tile_stackeddirectionalconv3d_t_kernel(tc, x, W, grad_out, out):
         mx(2, 2, 1, 5)
         mx(2, 3, 0, 6)
         mx(2, 3, 1, 7)
+        rw(3, 0, 0, 512, False)
         mr(1)
         rw(4, 0, 0, 512, False)
-        sc(0)
         qw(3, 0, 0, 512)
         mx(3, 0, 0, 0)
         mx(3, 0, 1, 1)
@@ -261,6 +257,7 @@ def tile_stackeddirectionalconv3d_t_kernel(tc, x, W, grad_out, out):
         mx(3, 2, 1, 5)
         mx(3, 3, 0, 6)
         mx(3, 3, 1, 7)
+        sc(0)
         qc(0)
         rw(5, 0, 0, 512, False)
         qw(4, 0, 0, 512)
@@ -302,22 +299,22 @@ def tile_stackeddirectionalconv3d_t_kernel(tc, x, W, grad_out, out):
         ev(0, 1, False)
         ev(1, 0, False)
         ev(1, 1, False)
-        ev(2, 0, False)
-        ev(2, 1, False)
         mx(0, 4, 0, 0)
         mx(0, 4, 1, 1)
         mx(0, 5, 0, 2)
         mx(0, 5, 1, 3)
-        mx(0, 6, 0, 4)
-        mx(0, 6, 1, 5)
-        ev(3, 0, False)
-        ev(3, 1, False)
         mx(1, 4, 0, 0)
         mx(1, 4, 1, 1)
         mx(1, 5, 0, 2)
         mx(1, 5, 1, 3)
+        ev(2, 0, False)
+        ev(2, 1, False)
+        mx(0, 6, 0, 4)
+        mx(0, 6, 1, 5)
         mx(1, 6, 0, 4)
         mx(1, 6, 1, 5)
+        ev(3, 0, False)
+        ev(3, 1, False)
         rw(3, 1, 0, 512, True)
         qw(2, 1, 0, 512)
         mx(2, 4, 0, 0)
@@ -326,7 +323,8 @@ def tile_stackeddirectionalconv3d_t_kernel(tc, x, W, grad_out, out):
         mx(2, 5, 1, 3)
         mx(2, 6, 0, 4)
         mx(2, 6, 1, 5)
-        rw(4, 1, 0, 512, True)
+        rw(4, 1, 0, 256, False)
+        rw(4, 1, 256, 512, True)
         qw(3, 1, 0, 512)
         mx(3, 4, 0, 0)
         mx(3, 4, 1, 1)
@@ -334,7 +332,8 @@ def tile_stackeddirectionalconv3d_t_kernel(tc, x, W, grad_out, out):
         mx(3, 5, 1, 3)
         mx(3, 6, 0, 4)
         mx(3, 6, 1, 5)
-        rw(5, 1, 0, 512, True)
+        rw(5, 1, 0, 256, False)
+        rw(5, 1, 256, 512, True)
         qw(4, 1, 0, 512)
         mx(4, 4, 0, 0)
         mx(4, 4, 1, 1)
@@ -342,7 +341,8 @@ def tile_stackeddirectionalconv3d_t_kernel(tc, x, W, grad_out, out):
         mx(4, 5, 1, 3)
         mx(4, 6, 0, 4)
         mx(4, 6, 1, 5)
-        rw(6, 1, 0, 512, True)
+        rw(6, 1, 0, 256, False)
+        rw(6, 1, 256, 512, True)
         qw(5, 1, 0, 512)
         mx(5, 4, 0, 0)
         mx(5, 4, 1, 1)

@@ -19,7 +19,7 @@ VOX = 512
 NDIR = 7
 HALF = 512
 PAD = 64
-SPLANE = 768
+SLOT = 256
 WOFF = 48
 
 FLOPS = 2 * NB * VOX * COUT * NDIR * CIN
@@ -49,7 +49,10 @@ def tile_stackeddirectionalconv3d_t_kernel(tc, x, W, grad_out, out):
             for d in range(2)
         ]
         base_c = keep.tile([P, NB, VOX + 2 * PAD], U32, name="base_c", align_bytes=256)
-        base_s = keep.tile([P, NB, SPLANE], U8, name="base_s", align_bytes=256)
+        t_s = [
+            keep.tile([P, NB, VOX], U8, name="t_s%d" % d, align_bytes=256)
+            for d in range(3)
+        ]
         dir_c = [
             keep.tile([P, NB, VOX], U32, name="dir_c%d" % d, align_bytes=256)
             for d in range(4)
@@ -65,20 +68,22 @@ def tile_stackeddirectionalconv3d_t_kernel(tc, x, W, grad_out, out):
             for k in range(NDIR):
                 w_raw[(k, h)] = keep.tile([P, PACK, HALF], BF16, name="w_raw%d_%d" % (k, h))
                 w_c[(k, h)] = keep.tile([P, WOFF + HALF], U32, name="w_c%d_%d" % (k, h), align_bytes=256)
-                w_s[(k, h)] = keep.tile([P, HALF], U8, name="w_s%d_%d" % (k, h), align_bytes=256)
+                w_s[(k, h)] = keep.tile([P, 4 * SLOT], U8, name="w_s%d_%d" % (k, h), align_bytes=256)
         w_grp = {}
         acc = {}
 
         base_c32 = base_c[:].bitcast(I32)
-        base_s32 = base_s[:].bitcast(I32)
+        t_s32 = [t_s[d][:].bitcast(I32) for d in range(3)]
         data_c32 = base_c32[:, :, PAD : PAD + VOX].rearrange("p b (t q) -> p b t q", q=64)
-        data_s32 = base_s32[:, :, PAD // 4 : (PAD + VOX) // 4].rearrange("p b (t q) -> p b t q", q=16)
+        data_s32 = t_s32[0].rearrange("p b (t q) -> p b t q", q=16)
         dir_c32 = [dir_c[d][:].bitcast(I32).rearrange("p b (t q) -> p b t q", q=64) for d in range(2)]
         dir_s32 = [dir_s[d][:].bitcast(I32).rearrange("p b (t q) -> p b t q", q=16) for d in range(2)]
         grp_rows = g_grp[:].rearrange("p b (a c) j -> p (b a) (c j)", c=8)
         sh_rows = [g_sh[d][:].rearrange("p b (a c) j -> p (b a) (c j)", c=8) for d in range(2)]
 
-        nc.vector.memset(base_s32, 0)
+        nc.vector.memset(t_s32[0], 0)
+        nc.vector.memset(t_s32[1][:, :, (VOX - PAD) // 4 : VOX // 4], 0)
+        nc.vector.memset(t_s32[2][:, :, 0 : PAD // 4], 0)
         nc.vector.memset(base_c32[:, :, 0:PAD], 0)
         nc.vector.memset(base_c32[:, :, PAD + VOX : PAD + VOX + PAD], 0)
         nc.vector.memset(dir_c32[0][:, :, :, 56:64], 0)
@@ -109,9 +114,19 @@ def tile_stackeddirectionalconv3d_t_kernel(tc, x, W, grad_out, out):
         def qg(b, v0, v1):
             nc.vector.quantize_mx(
                 out=base_c[:, b, PAD + v0 : PAD + v1].bitcast(E5M2X4),
-                scales=base_s[:, b, PAD + v0 : PAD + v1],
+                scales=t_s[0][:, b, v0:v1],
                 in_=g_grp[:, b, v0:v1, :].rearrange("p w j -> p (w j)"),
             )
+
+        def mt(d):
+            if d == 1:
+                nc.vector.tensor_copy(
+                    out=t_s32[1][:, :, 0 : (VOX - PAD) // 4], in_=t_s32[0][:, :, PAD // 4 : VOX // 4]
+                )
+            else:
+                nc.vector.tensor_copy(
+                    out=t_s32[2][:, :, PAD // 4 : VOX // 4], in_=t_s32[0][:, :, 0 : (VOX - PAD) // 4]
+                )
 
         def mr(d):
             if d == 0:
@@ -142,31 +157,31 @@ def tile_stackeddirectionalconv3d_t_kernel(tc, x, W, grad_out, out):
             regroup(on_vector, w_grp[(k, h)][:, c0:c1, :], w_raw[(k, h)][:, :, c0:c1])
 
         def qw(k, h, c0, c1):
-            nc.vector.quantize_mx(
-                out=w_c[(k, h)][:, WOFF + c0 : WOFF + c1].bitcast(E4M3X4),
-                scales=w_s[(k, h)][:, c0:c1],
-                in_=w_grp[(k, h)][:, c0:c1, :].rearrange("p w j -> p (w j)"),
-            )
+            for mm in range(c0 // P, c1 // P):
+                nc.vector.quantize_mx(
+                    out=w_c[(k, h)][:, WOFF + mm * P : WOFF + (mm + 1) * P].bitcast(E4M3X4),
+                    scales=w_s[(k, h)][:, mm * SLOT : mm * SLOT + P],
+                    in_=w_grp[(k, h)][:, mm * P : (mm + 1) * P, :].rearrange("p w j -> p (w j)"),
+                )
 
         def moving(k, b):
             if k == 0:
-                return base_c[:, b, PAD : PAD + VOX], base_s[:, b, PAD : PAD + VOX]
+                return base_c[:, b, PAD : PAD + VOX], t_s[0][:, b, :]
             if k == 1:
-                return base_c[:, b, 2 * PAD : 2 * PAD + VOX], base_s[:, b, 2 * PAD : 2 * PAD + VOX]
+                return base_c[:, b, 2 * PAD : 2 * PAD + VOX], t_s[1][:, b, :]
             if k == 2:
-                return base_c[:, b, 0:VOX], base_s[:, b, 0:VOX]
+                return base_c[:, b, 0:VOX], t_s[2][:, b, :]
             return dir_c[k - 3][:, b, :], dir_s[k - 3][:, b, :]
 
         def mx(k, m, b, bank):
             if k == 0:
                 acc[(m, b)] = psum.tile([P, VOX], F32, tag="bank%d" % bank, name="acc%d_%d" % (m, b))
             h = m // 4
-            cols = slice((m % 4) * P, (m % 4 + 1) * P)
             codes, scales = moving(k, b)
             nc.tensor.matmul_mx(
                 out=acc[(m, b)][:],
                 lhsT=w_c[(k, h)][:, WOFF + (m % 4) * P : WOFF + (m % 4 + 1) * P].bitcast(E4M3X4),
-                lhsT_scale=w_s[(k, h)][:, cols],
+                lhsT_scale=w_s[(k, h)][:, (m % 4) * SLOT : (m % 4) * SLOT + P],
                 rhs=codes.bitcast(E5M2X4),
                 rhs_scale=scales,
                 start=(k == 0),
@@ -213,11 +228,13 @@ def tile_stackeddirectionalconv3d_t_kernel(tc, x, W, grad_out, out):
         qg(1, 0, 256)
         qg(1, 256, 512)
         qw(0, 0, 384, 512)
+        mt(1)
         rw(1, 0, 0, 256, False)
         rw(1, 0, 256, 512, True)
         rw(2, 0, 0, 384, False)
         qw(1, 0, 0, 256)
         qw(1, 0, 256, 512)
+        mt(2)
         rw(2, 0, 384, 512, True)
         mr(0)
         qw(2, 0, 0, 512)

@@ -25,7 +25,7 @@ WOFF = 48
 FLOPS = 2 * NB * VOX * COUT * NDIR * CIN
 BYTES = NDIR * COUT * CIN * 2 + NB * COUT * VOX * 2 + NB * CIN * VOX * 4
 
-MANUAL = True
+MANUAL = False
 
 
 def tile_stackeddirectionalconv3d_t_kernel(tc, x, W, grad_out, out):

@@ -25,7 +25,7 @@ WOFF = 48
 FLOPS = 2 * NB * VOX * COUT * NDIR * CIN
 BYTES = NDIR * COUT * CIN * 2 + NB * COUT * VOX * 2 + NB * CIN * VOX * 4
 
-MANUAL = False
+MANUAL = True
 
 
 def tile_stackeddirectionalconv3d_t_kernel(tc, x, W, grad_out, out):
@@ -262,9 +262,11 @@ def tile_stackeddirectionalconv3d_t_kernel(tc, x, W, grad_out, out):
         mx(2, 2, 1, 5)
         mx(2, 3, 0, 6)
         mx(2, 3, 1, 7)
-        rw(3, 0, 0, 512, False)
+        rw(3, 0, 0, 448, False)
+        rw(3, 0, 448, 512, True)
         mr(1)
         rw(4, 0, 0, 512, False)
+        sc(0)
         qw(3, 0, 0, 512)
         mx(3, 0, 0, 0)
         mx(3, 0, 1, 1)
@@ -274,9 +276,9 @@ def tile_stackeddirectionalconv3d_t_kernel(tc, x, W, grad_out, out):
         mx(3, 2, 1, 5)
         mx(3, 3, 0, 6)
         mx(3, 3, 1, 7)
-        sc(0)
         qc(0)
-        rw(5, 0, 0, 512, False)
+        rw(5, 0, 0, 448, False)
+        rw(5, 0, 448, 512, True)
         qw(4, 0, 0, 512)
         mx(4, 0, 0, 0)
         mx(4, 0, 1, 1)
@@ -299,7 +301,6 @@ def tile_stackeddirectionalconv3d_t_kernel(tc, x, W, grad_out, out):
         mx(5, 3, 1, 7)
         qc(1)
         rw(0, 1, 0, 512, False)
-        rw(1, 1, 0, 512, True)
         qw(6, 0, 0, 512)
         mx(6, 0, 0, 0)
         mx(6, 0, 1, 1)
@@ -309,6 +310,7 @@ def tile_stackeddirectionalconv3d_t_kernel(tc, x, W, grad_out, out):
         mx(6, 2, 1, 5)
         mx(6, 3, 0, 6)
         mx(6, 3, 1, 7)
+        rw(1, 1, 0, 512, True)
         qw(0, 1, 0, 512)
         rw(2, 1, 0, 512, True)
         qw(1, 1, 0, 512)

@@ -37,17 +37,13 @@ def tile_stackeddirectionalconv3d_t_kernel(tc, x, W, grad_out, out):
     with ExitStack() as ctx:
         keep = ctx.enter_context(tc.tile_pool(name="keep", bufs=1))
         stage = ctx.enter_context(tc.tile_pool(name="stage", bufs=4))
-        outp = ctx.enter_context(tc.tile_pool(name="outp", bufs=6))
+        outp = ctx.enter_context(tc.tile_pool(name="outp", bufs=16))
         psum = ctx.enter_context(tc.psum_pool(name="psum", bufs=1))
         if MANUAL:
             ctx.enter_context(tc.manual_schedule())
 
         g_raw = keep.tile([P, NB, PACK, VOX], BF16, name="g_raw")
         g_grp = keep.tile([P, NB, VOX, PACK], BF16, name="g_grp", align_bytes=64)
-        g_sh = [
-            keep.tile([P, NB, VOX, PACK], BF16, name="g_sh%d" % d, align_bytes=64)
-            for d in range(2)
-        ]
         base_c = keep.tile([P, NB, VOX + 2 * PAD], U32, name="base_c", align_bytes=256)
         t_s = [
             keep.tile([P, NB, VOX], U8, name="t_s%d" % d, align_bytes=256)
@@ -78,8 +74,10 @@ def tile_stackeddirectionalconv3d_t_kernel(tc, x, W, grad_out, out):
         data_s32 = t_s32[0].rearrange("p b (t q) -> p b t q", q=16)
         dir_c32 = [dir_c[d][:].bitcast(I32).rearrange("p b (t q) -> p b t q", q=64) for d in range(2)]
         dir_s32 = [dir_s[d][:].bitcast(I32).rearrange("p b (t q) -> p b t q", q=16) for d in range(2)]
-        grp_rows = g_grp[:].rearrange("p b (a c) j -> p (b a) (c j)", c=8)
-        sh_rows = [g_sh[d][:].rearrange("p b (a c) j -> p (b a) (c j)", c=8) for d in range(2)]
+        row_c32 = base_c32[:, :, PAD : PAD + VOX].rearrange("p b (a c) -> p b a c", c=8)
+        row_s8 = t_s[0][:].rearrange("p b (a c) -> p (b a) c", c=8)
+        col_c32 = [dir_c[2 + d][:].bitcast(I32).rearrange("p b (a c) -> p b a c", c=8) for d in range(2)]
+        col_s8 = [dir_s[2 + d][:].rearrange("p b (a c) -> p (b a) c", c=8) for d in range(2)]
 
         nc.vector.memset(t_s32[0], 0)
         nc.vector.memset(t_s32[1][:, :, (VOX - PAD) // 4 : VOX // 4], 0)
@@ -90,8 +88,10 @@ def tile_stackeddirectionalconv3d_t_kernel(tc, x, W, grad_out, out):
         nc.vector.memset(dir_c32[1][:, :, :, 0:8], 0)
         nc.vector.memset(dir_s32[0][:, :, :, 14:16], 0)
         nc.vector.memset(dir_s32[1][:, :, :, 0:2], 0)
-        nc.vector.memset(sh_rows[0][:, :, 28:32], 0.0)
-        nc.vector.memset(sh_rows[1][:, :, 0:4], 0.0)
+        nc.vector.memset(col_c32[0][:, :, :, 7:8], 0)
+        nc.vector.memset(col_c32[1][:, :, :, 0:1], 0)
+        nc.vector.memset(dir_s[2][:].bitcast(I32), 0)
+        nc.vector.memset(dir_s[3][:].bitcast(I32), 0)
 
         def lw(k, h, c0, c1):
             nc.sync.dma_start(
@@ -138,16 +138,15 @@ def tile_stackeddirectionalconv3d_t_kernel(tc, x, W, grad_out, out):
 
         def sc(d):
             if d == 0:
-                nc.vector.tensor_copy(out=sh_rows[0][:, :, 0:28], in_=grp_rows[:, :, 4:32])
+                nc.vector.tensor_copy(out=col_c32[0][:, :, :, 0:7], in_=row_c32[:, :, :, 1:8])
             else:
-                nc.vector.tensor_copy(out=sh_rows[1][:, :, 4:32], in_=grp_rows[:, :, 0:28])
+                nc.vector.tensor_copy(out=col_c32[1][:, :, :, 1:8], in_=row_c32[:, :, :, 0:7])
 
         def qc(d):
-            nc.vector.quantize_mx(
-                out=dir_c[2 + d][:].rearrange("p b v -> p (b v)").bitcast(E5M2X4),
-                scales=dir_s[2 + d][:].rearrange("p b v -> p (b v)"),
-                in_=g_sh[d][:].rearrange("p b w j -> p (b w j)"),
-            )
+            if d == 0:
+                nc.vector.tensor_copy(out=col_s8[0][:, :, 0:7], in_=row_s8[:, :, 1:8])
+            else:
+                nc.vector.tensor_copy(out=col_s8[1][:, :, 1:8], in_=row_s8[:, :, 0:7])
 
         def rw(k, h, c0, c1, on_vector):
             if (k, h) not in w_grp:
@@ -196,205 +195,86 @@ def tile_stackeddirectionalconv3d_t_kernel(tc, x, W, grad_out, out):
                 nc.scalar.copy(out=res[:], in_=acc[(m, b)][:])
             nc.sync.dma_start(out=o_view[b, m], in_=res[:])
 
+        S_COLS = [0, 320, 320, 320, 320, 320, 320, 320, 0, 0, 0, 256, 256, 256]
+
+        def rw_split(n):
+            k, h = n % NDIR, n // NDIR
+            if S_COLS[n] > 0:
+                rw(k, h, 0, S_COLS[n], False)
+            if S_COLS[n] < HALF:
+                rw(k, h, S_COLS[n], HALF, True)
+
+        def prep(k):
+            if k == 1 or k == 2:
+                mt(k)
+            elif k == 3 or k == 4:
+                mr(k - 3)
+            elif k == 5 or k == 6:
+                sc(k - 5)
+                qc(k - 5)
+
         lg(0, 0, 512)
         lw(0, 0, 0, 512)
         lg(1, 0, 512)
-        lw(1, 0, 0, 512)
-        lw(2, 0, 0, 512)
-        lw(3, 0, 0, 512)
-        lw(4, 0, 0, 512)
-        lw(5, 0, 0, 512)
-        lw(6, 0, 0, 512)
-        lw(0, 1, 0, 512)
-        lw(1, 1, 0, 512)
-        lw(2, 1, 0, 512)
-        lw(3, 1, 0, 512)
-        lw(4, 1, 0, 512)
-        lw(5, 1, 0, 512)
-        lw(6, 1, 0, 512)
-        rg(0, 0, 256, True)
+        for n in range(1, 2 * NDIR):
+            lw(n % NDIR, n // NDIR, 0, 512)
+        rg(0, 0, 320, True)
+        rg(0, 320, 512, False)
+        qg(0, 0, 512)
         rw(0, 0, 0, 128, False)
-        rg(0, 256, 512, True)
         rw(0, 0, 128, 256, False)
-        qg(0, 0, 256)
-        qg(0, 256, 512)
+        rw(0, 0, 256, 384, True)
         qw(0, 0, 0, 128)
-        rw(0, 0, 256, 384, False)
-        rg(1, 0, 256, True)
-        qw(0, 0, 128, 256)
-        rw(0, 0, 384, 512, False)
-        rg(1, 256, 512, True)
+        rw(0, 0, 384, 512, True)
         qw(0, 0, 256, 384)
-        qg(1, 0, 256)
-        qg(1, 256, 512)
+        qw(0, 0, 128, 256)
         qw(0, 0, 384, 512)
-        mt(1)
-        rw(1, 0, 0, 256, False)
-        rw(1, 0, 256, 512, True)
-        rw(2, 0, 0, 384, False)
-        qw(1, 0, 0, 256)
-        qw(1, 0, 256, 512)
-        mt(2)
-        rw(2, 0, 384, 512, True)
-        mr(0)
-        qw(2, 0, 0, 512)
-        mx(0, 0, 0, 0)
-        mx(0, 1, 0, 2)
-        mx(0, 2, 0, 4)
-        mx(0, 0, 1, 1)
-        mx(0, 1, 1, 3)
-        mx(0, 2, 1, 5)
-        mx(0, 3, 0, 6)
-        mx(0, 3, 1, 7)
-        mx(1, 0, 0, 0)
-        mx(1, 0, 1, 1)
-        mx(1, 1, 0, 2)
-        mx(1, 1, 1, 3)
-        mx(1, 2, 0, 4)
-        mx(1, 2, 1, 5)
-        mx(1, 3, 0, 6)
-        mx(1, 3, 1, 7)
-        mx(2, 0, 0, 0)
-        mx(2, 0, 1, 1)
-        mx(2, 1, 0, 2)
-        mx(2, 1, 1, 3)
-        mx(2, 2, 0, 4)
-        mx(2, 2, 1, 5)
-        mx(2, 3, 0, 6)
-        mx(2, 3, 1, 7)
-        rw(3, 0, 0, 448, False)
-        rw(3, 0, 448, 512, True)
-        mr(1)
-        rw(4, 0, 0, 512, False)
-        sc(0)
-        qw(3, 0, 0, 512)
-        mx(3, 0, 0, 0)
-        mx(3, 0, 1, 1)
-        mx(3, 1, 0, 2)
-        mx(3, 1, 1, 3)
-        mx(3, 2, 0, 4)
-        mx(3, 2, 1, 5)
-        mx(3, 3, 0, 6)
-        mx(3, 3, 1, 7)
-        qc(0)
-        rw(5, 0, 0, 448, False)
-        rw(5, 0, 448, 512, True)
-        qw(4, 0, 0, 512)
-        mx(4, 0, 0, 0)
-        mx(4, 0, 1, 1)
-        mx(4, 1, 0, 2)
-        mx(4, 1, 1, 3)
-        mx(4, 2, 0, 4)
-        mx(4, 2, 1, 5)
-        mx(4, 3, 0, 6)
-        mx(4, 3, 1, 7)
-        sc(1)
-        rw(6, 0, 0, 512, False)
-        qw(5, 0, 0, 512)
-        mx(5, 0, 0, 0)
-        mx(5, 0, 1, 1)
-        mx(5, 1, 0, 2)
-        mx(5, 1, 1, 3)
-        mx(5, 2, 0, 4)
-        mx(5, 2, 1, 5)
-        mx(5, 3, 0, 6)
-        mx(5, 3, 1, 7)
-        qc(1)
-        rw(0, 1, 0, 512, False)
-        qw(6, 0, 0, 512)
-        mx(6, 0, 0, 0)
-        mx(6, 0, 1, 1)
-        mx(6, 1, 0, 2)
-        mx(6, 1, 1, 3)
-        mx(6, 2, 0, 4)
-        mx(6, 2, 1, 5)
-        mx(6, 3, 0, 6)
-        mx(6, 3, 1, 7)
-        rw(1, 1, 0, 512, True)
+        rg(1, 256, 512, False)
+        rg(1, 0, 256, True)
+        qg(1, 0, 512)
+        rw_split(1)
+        for m in (0, 2, 1, 3):
+            mx(0, m, 0, 2 * m)
+        for m in (0, 2, 1, 3):
+            mx(0, m, 1, 2 * m + 1)
+        for k in range(1, NDIR):
+            prep(k)
+            qw(k, 0, 0, 512)
+            rw_split(k + 1)
+            for m in range(4):
+                for b in range(NB):
+                    mx(k, m, b, 2 * m + b)
         qw(0, 1, 0, 512)
-        rw(2, 1, 0, 512, True)
+        rw_split(NDIR + 1)
         qw(1, 1, 0, 512)
-        ev(0, 0, False)
-        ev(0, 1, False)
-        ev(1, 0, False)
-        ev(1, 1, False)
-        mx(0, 4, 0, 0)
-        mx(0, 4, 1, 1)
-        mx(0, 5, 0, 2)
-        mx(0, 5, 1, 3)
-        mx(1, 4, 0, 0)
-        mx(1, 4, 1, 1)
-        mx(1, 5, 0, 2)
-        mx(1, 5, 1, 3)
-        ev(2, 0, False)
-        ev(2, 1, False)
-        mx(0, 6, 0, 4)
-        mx(0, 6, 1, 5)
-        mx(1, 6, 0, 4)
-        mx(1, 6, 1, 5)
-        ev(3, 0, False)
-        ev(3, 1, False)
-        rw(3, 1, 0, 512, True)
-        qw(2, 1, 0, 512)
-        mx(2, 4, 0, 0)
-        mx(2, 4, 1, 1)
-        mx(2, 5, 0, 2)
-        mx(2, 5, 1, 3)
-        mx(2, 6, 0, 4)
-        mx(2, 6, 1, 5)
-        rw(4, 1, 0, 256, False)
-        rw(4, 1, 256, 512, True)
-        qw(3, 1, 0, 512)
-        mx(3, 4, 0, 0)
-        mx(3, 4, 1, 1)
-        mx(3, 5, 0, 2)
-        mx(3, 5, 1, 3)
-        mx(3, 6, 0, 4)
-        mx(3, 6, 1, 5)
-        rw(5, 1, 0, 256, False)
-        rw(5, 1, 256, 512, True)
-        qw(4, 1, 0, 512)
-        mx(4, 4, 0, 0)
-        mx(4, 4, 1, 1)
-        mx(4, 5, 0, 2)
-        mx(4, 5, 1, 3)
-        mx(4, 6, 0, 4)
-        mx(4, 6, 1, 5)
-        rw(6, 1, 0, 256, False)
-        rw(6, 1, 256, 512, True)
-        qw(5, 1, 0, 512)
-        mx(5, 4, 0, 0)
-        mx(5, 4, 1, 1)
-        mx(5, 5, 0, 2)
-        mx(5, 5, 1, 3)
-        mx(5, 6, 0, 4)
-        mx(5, 6, 1, 5)
-        qw(6, 1, 0, 512)
-        mx(6, 4, 0, 0)
-        mx(6, 4, 1, 1)
-        mx(6, 5, 0, 2)
-        mx(6, 5, 1, 3)
-        mx(6, 6, 0, 4)
-        mx(6, 6, 1, 5)
-        mx(0, 7, 0, 6)
-        mx(1, 7, 0, 6)
-        mx(2, 7, 0, 6)
-        mx(3, 7, 0, 6)
-        mx(4, 7, 0, 6)
-        mx(5, 7, 0, 6)
-        mx(6, 7, 0, 6)
-        ev(4, 0, False)
-        ev(4, 1, True)
-        ev(5, 0, False)
-        ev(5, 1, True)
-        ev(6, 0, False)
-        ev(6, 1, True)
+        rw_split(NDIR + 2)
+        for m in range(2):
+            for b in range(NB):
+                ev(m, b, False)
+        for k in range(2):
+            for m in range(4, 6):
+                for b in range(NB):
+                    mx(k, m, b, 2 * (m - 4) + b)
+        for b in range(NB):
+            ev(2, b, False)
+        for k in range(2):
+            for b in range(NB):
+                mx(k, 6, b, 4 + b)
+        for b in range(NB):
+            ev(3, b, False)
+        for k in range(2, NDIR):
+            qw(k, 1, 0, 512)
+            if k + 1 < NDIR:
+                rw_split(NDIR + k + 1)
+            for m in range(4, 7):
+                for b in range(NB):
+                    mx(k, m, b, 2 * (m - 4) + b)
+        for k in range(NDIR):
+            mx(k, 7, 0, 6)
+        for m in range(4, 7):
+            ev(m, 0, False)
+            ev(m, 1, True)
         ev(7, 0, True)
-        mx(0, 7, 1, 7)
-        mx(1, 7, 1, 7)
-        mx(2, 7, 1, 7)
-        mx(3, 7, 1, 7)
-        mx(4, 7, 1, 7)
-        mx(5, 7, 1, 7)
-        mx(6, 7, 1, 7)
+        for k in range(NDIR):
+            mx(k, 7, 1, 7)
         ev(7, 1, False)

@@ -19,7 +19,7 @@ VOX = 512
 NDIR = 7
 HALF = 512
 PAD = 64
-SLOT = 256
+SLOT = 128
 WOFF = 48
 
 FLOPS = 2 * NB * VOX * COUT * NDIR * CIN
@@ -156,12 +156,11 @@ def tile_stackeddirectionalconv3d_t_kernel(tc, x, W, grad_out, out):
             regroup(on_vector, w_grp[(k, h)][:, c0:c1, :], w_raw[(k, h)][:, :, c0:c1])
 
         def qw(k, h, c0, c1):
-            for mm in range(c0 // P, c1 // P):
-                nc.vector.quantize_mx(
-                    out=w_c[(k, h)][:, WOFF + mm * P : WOFF + (mm + 1) * P].bitcast(E4M3X4),
-                    scales=w_s[(k, h)][:, mm * SLOT : mm * SLOT + P],
-                    in_=w_grp[(k, h)][:, mm * P : (mm + 1) * P, :].rearrange("p w j -> p (w j)"),
-                )
+            nc.vector.quantize_mx(
+                out=w_c[(k, h)][:, WOFF + c0 : WOFF + c1].bitcast(E4M3X4),
+                scales=w_s[(k, h)][:, c0:c1],
+                in_=w_grp[(k, h)][:, c0:c1, :].rearrange("p w j -> p (w j)"),
+            )
 
         def moving(k, b):
             if k == 0:
@@ -239,7 +238,11 @@ def tile_stackeddirectionalconv3d_t_kernel(tc, x, W, grad_out, out):
             mx(0, m, 1, 2 * m + 1)
         for k in range(1, NDIR):
             prep(k)
-            qw(k, 0, 0, 512)
+            if k == 1:
+                for c0 in range(0, HALF, P):
+                    qw(k, 0, c0, c0 + P)
+            else:
+                qw(k, 0, 0, 512)
             rw_split(k + 1)
             for m in range(4):
                 for b in range(NB):

@@ -45,10 +45,7 @@ def tile_stackeddirectionalconv3d_t_kernel(tc, x, W, grad_out, out):
         g_raw = keep.tile([P, NB, PACK, VOX], BF16, name="g_raw")
         g_grp = keep.tile([P, NB, VOX, PACK], BF16, name="g_grp", align_bytes=64)
         base_c = keep.tile([P, NB, VOX + 2 * PAD], U32, name="base_c", align_bytes=256)
-        t_s = [
-            keep.tile([P, NB, VOX], U8, name="t_s%d" % d, align_bytes=256)
-            for d in range(3)
-        ]
+        base_s = keep.tile([P, NB, VOX + 2 * PAD], U8, name="base_s", align_bytes=256)
         dir_c = [
             keep.tile([P, NB, VOX], U32, name="dir_c%d" % d, align_bytes=256)
             for d in range(4)
@@ -67,21 +64,21 @@ def tile_stackeddirectionalconv3d_t_kernel(tc, x, W, grad_out, out):
                 w_s[(k, h)] = keep.tile([P, 4 * SLOT], U8, name="w_s%d_%d" % (k, h), align_bytes=256)
         w_grp = {}
         acc = {}
+        zeros = keep.tile([P, VOX], BF16, name="zeros")
+        nc.vector.memset(zeros[:], 0.0)
 
         base_c32 = base_c[:].bitcast(I32)
-        t_s32 = [t_s[d][:].bitcast(I32) for d in range(3)]
+        base_s32 = base_s[:].bitcast(I32)
         data_c32 = base_c32[:, :, PAD : PAD + VOX].rearrange("p b (t q) -> p b t q", q=64)
-        data_s32 = t_s32[0].rearrange("p b (t q) -> p b t q", q=16)
+        data_s32 = base_s32[:, :, PAD // 4 : (PAD + VOX) // 4].rearrange("p b (t q) -> p b t q", q=16)
         dir_c32 = [dir_c[d][:].bitcast(I32).rearrange("p b (t q) -> p b t q", q=64) for d in range(2)]
         dir_s32 = [dir_s[d][:].bitcast(I32).rearrange("p b (t q) -> p b t q", q=16) for d in range(2)]
         row_c32 = base_c32[:, :, PAD : PAD + VOX].rearrange("p b (a c) -> p b a c", c=8)
-        row_s8 = t_s[0][:].rearrange("p b (a c) -> p (b a) c", c=8)
+        row_s8 = base_s[:, :, PAD : PAD + VOX].rearrange("p b (a c) -> p b a c", c=8)
         col_c32 = [dir_c[2 + d][:].bitcast(I32).rearrange("p b (a c) -> p b a c", c=8) for d in range(2)]
-        col_s8 = [dir_s[2 + d][:].rearrange("p b (a c) -> p (b a) c", c=8) for d in range(2)]
+        col_s8 = [dir_s[2 + d][:].rearrange("p b (a c) -> p b a c", c=8) for d in range(2)]
 
-        nc.vector.memset(t_s32[0], 0)
-        nc.vector.memset(t_s32[1][:, :, (VOX - PAD) // 4 : VOX // 4], 0)
-        nc.vector.memset(t_s32[2][:, :, 0 : PAD // 4], 0)
+        nc.vector.memset(base_s32, 0)
         nc.vector.memset(base_c32[:, :, 0:PAD], 0)
         nc.vector.memset(base_c32[:, :, PAD + VOX : PAD + VOX + PAD], 0)
         nc.vector.memset(dir_c32[0][:, :, :, 56:64], 0)
@@ -114,19 +111,9 @@ def tile_stackeddirectionalconv3d_t_kernel(tc, x, W, grad_out, out):
         def qg(b, v0, v1):
             nc.vector.quantize_mx(
                 out=base_c[:, b, PAD + v0 : PAD + v1].bitcast(E5M2X4),
-                scales=t_s[0][:, b, v0:v1],
+                scales=base_s[:, b, PAD + v0 : PAD + v1],
                 in_=g_grp[:, b, v0:v1, :].rearrange("p w j -> p (w j)"),
             )
-
-        def mt(d):
-            if d == 1:
-                nc.vector.tensor_copy(
-                    out=t_s32[1][:, :, 0 : (VOX - PAD) // 4], in_=t_s32[0][:, :, PAD // 4 : VOX // 4]
-                )
-            else:
-                nc.vector.tensor_copy(
-                    out=t_s32[2][:, :, PAD // 4 : VOX // 4], in_=t_s32[0][:, :, 0 : (VOX - PAD) // 4]
-                )
 
         def mr(d):
             if d == 0:
@@ -144,9 +131,9 @@ def tile_stackeddirectionalconv3d_t_kernel(tc, x, W, grad_out, out):
 
         def qc(d):
             if d == 0:
-                nc.vector.tensor_copy(out=col_s8[0][:, :, 0:7], in_=row_s8[:, :, 1:8])
+                nc.vector.tensor_copy(out=col_s8[0][:, :, :, 0:7], in_=row_s8[:, :, :, 1:8])
             else:
-                nc.vector.tensor_copy(out=col_s8[1][:, :, 1:8], in_=row_s8[:, :, 0:7])
+                nc.vector.tensor_copy(out=col_s8[1][:, :, :, 1:8], in_=row_s8[:, :, :, 0:7])
 
         def rw(k, h, c0, c1, on_vector):
             if (k, h) not in w_grp:
@@ -163,12 +150,9 @@ def tile_stackeddirectionalconv3d_t_kernel(tc, x, W, grad_out, out):
             )
 
         def moving(k, b):
-            if k == 0:
-                return base_c[:, b, PAD : PAD + VOX], t_s[0][:, b, :]
-            if k == 1:
-                return base_c[:, b, 2 * PAD : 2 * PAD + VOX], t_s[1][:, b, :]
-            if k == 2:
-                return base_c[:, b, 0:VOX], t_s[2][:, b, :]
+            if k < 3:
+                v0 = (PAD, 2 * PAD, 0)[k]
+                return base_c[:, b, v0 : v0 + VOX], base_s[:, b, v0 : v0 + VOX]
             return dir_c[k - 3][:, b, :], dir_s[k - 3][:, b, :]
 
         def mx(k, m, b, bank):
@@ -194,7 +178,7 @@ def tile_stackeddirectionalconv3d_t_kernel(tc, x, W, grad_out, out):
                 nc.scalar.copy(out=res[:], in_=acc[(m, b)][:])
             nc.sync.dma_start(out=o_view[b, m], in_=res[:])
 
-        S_COLS = [0, 320, 320, 320, 320, 320, 320, 320, 0, 0, 0, 256, 256, 256]
+        S_COLS = [0, 320, 320, 320, 320, 384, 384, 384, 256, 128, 0, 256, 256, 256]
 
         def rw_split(n):
             k, h = n % NDIR, n // NDIR
@@ -204,9 +188,7 @@ def tile_stackeddirectionalconv3d_t_kernel(tc, x, W, grad_out, out):
                 rw(k, h, S_COLS[n], HALF, True)
 
         def prep(k):
-            if k == 1 or k == 2:
-                mt(k)
-            elif k == 3 or k == 4:
+            if k == 3 or k == 4:
                 mr(k - 3)
             elif k == 5 or k == 6:
                 sc(k - 5)
@@ -217,6 +199,9 @@ def tile_stackeddirectionalconv3d_t_kernel(tc, x, W, grad_out, out):
         lg(1, 0, 512)
         for n in range(1, 2 * NDIR):
             lw(n % NDIR, n // NDIR, 0, 512)
+        warm = psum.tile([P, VOX], F32, tag="bank7", name="warm")
+        for i in range(10):
+            nc.tensor.matmul(warm[:], lhsT=zeros[:, 0:P], rhs=zeros[:], start=True, stop=True)
         rg(0, 0, 320, True)
         rg(0, 320, 512, False)
         qg(0, 0, 512)
@@ -227,9 +212,9 @@ def tile_stackeddirectionalconv3d_t_kernel(tc, x, W, grad_out, out):
         rw(0, 0, 384, 512, True)
         qw(0, 0, 256, 384)
         qw(0, 0, 128, 256)
-        qw(0, 0, 384, 512)
         rg(1, 256, 512, False)
         rg(1, 0, 256, True)
+        qw(0, 0, 384, 512)
         qg(1, 0, 512)
         rw_split(1)
         for m in (0, 2, 1, 3):

@@ -178,7 +178,7 @@ def tile_stackeddirectionalconv3d_t_kernel(tc, x, W, grad_out, out):
                 nc.scalar.copy(out=res[:], in_=acc[(m, b)][:])
             nc.sync.dma_start(out=o_view[b, m], in_=res[:])
 
-        S_COLS = [0, 320, 320, 320, 320, 384, 384, 384, 256, 128, 0, 256, 256, 256]
+        S_COLS = [0, 320, 192, 256, 320, 384, 384, 384, 0, 0, 0, 256, 256, 256]
 
         def rw_split(n):
             k, h = n % NDIR, n // NDIR
@@ -209,18 +209,22 @@ def tile_stackeddirectionalconv3d_t_kernel(tc, x, W, grad_out, out):
         rw(0, 0, 128, 256, False)
         rw(0, 0, 256, 384, True)
         qw(0, 0, 0, 128)
-        rw(0, 0, 384, 512, True)
         qw(0, 0, 256, 384)
+        rg(1, 320, 512, False)
+        rg(1, 0, 320, True)
         qw(0, 0, 128, 256)
-        rg(1, 256, 512, False)
-        rg(1, 0, 256, True)
-        qw(0, 0, 384, 512)
         qg(1, 0, 512)
-        rw_split(1)
-        for m in (0, 2, 1, 3):
+        rw(0, 0, 384, 512, False)
+        qw(0, 0, 384, 512)
+        rw(1, 0, 0, 128, False)
+        rw(1, 0, 128, 384, True)
+        rw(1, 0, 384, 512, False)
+        for m in (0, 2, 1):
             mx(0, m, 0, 2 * m)
-        for m in (0, 2, 1, 3):
+        for m in (0, 2, 1):
             mx(0, m, 1, 2 * m + 1)
+        for b in range(2):
+            mx(0, 3, b, 6 + b)
         for k in range(1, NDIR):
             prep(k)
             if k == 1:

@@ -200,8 +200,10 @@ def tile_stackeddirectionalconv3d_t_kernel(tc, x, W, grad_out, out):
         for n in range(1, 2 * NDIR):
             lw(n % NDIR, n // NDIR, 0, 512)
         warm = psum.tile([P, VOX], F32, tag="bank7", name="warm")
-        for i in range(10):
+        for i in range(7):
             nc.tensor.matmul(warm[:], lhsT=zeros[:, 0:P], rhs=zeros[:], start=True, stop=True)
+        for i in range(5):
+            nc.tensor.matmul(warm[:], lhsT=zeros[:, 0:P], rhs=g_raw[:, 0, i % PACK, :], start=True, stop=True)
         rg(0, 0, 320, True)
         rg(0, 320, 512, False)
         qg(0, 0, 512)

@@ -21,6 +21,7 @@ HALF = 512
 PAD = 64
 SLOT = 128
 WOFF = 48
+WHOLE = 5
 
 FLOPS = 2 * NB * VOX * COUT * NDIR * CIN
 BYTES = NDIR * COUT * CIN * 2 + NB * COUT * VOX * 2 + NB * CIN * VOX * 4
@@ -32,12 +33,12 @@ def tile_stackeddirectionalconv3d_t_kernel(tc, x, W, grad_out, out):
     nc = tc.nc
     w_view = W.rearrange("(k p j) i -> k p j i", k=NDIR, j=PACK)
     g_view = grad_out.rearrange("b (p j) t r c -> b p j (t r c)", j=PACK)
-    o_view = out.rearrange("b (m p) t r c -> b m p (t r c)", p=P)
+    o_view = out.rearrange("b (m p) t r c -> m p b (t r c)", p=P)
 
     with ExitStack() as ctx:
         keep = ctx.enter_context(tc.tile_pool(name="keep", bufs=1))
         stage = ctx.enter_context(tc.tile_pool(name="stage", bufs=4))
-        outp = ctx.enter_context(tc.tile_pool(name="outp", bufs=16))
+        outp = ctx.enter_context(tc.tile_pool(name="outp", bufs=8))
         psum = ctx.enter_context(tc.psum_pool(name="psum", bufs=1))
         if MANUAL:
             ctx.enter_context(tc.manual_schedule())
@@ -55,11 +56,25 @@ def tile_stackeddirectionalconv3d_t_kernel(tc, x, W, grad_out, out):
             for d in range(4)
         ]
         w_raw = {}
+        w_first = []
+        for i in range(2):
+            piece = keep.tile([P, PACK, HALF // 2], BF16, name="w_first%d" % i)
+            w_first.append(piece[:])
         w_c = {}
         w_s = {}
+        for k in range(WHOLE):
+            for h in range(2):
+                if (k, h) == (0, 0):
+                    continue
+                half = keep.tile([P, PACK, HALF], BF16, name="w_raw%d_%d" % (k, h))
+                w_raw[(k, h)] = half[:]
+        for k in range(WHOLE, NDIR):
+            whole = keep.tile([P, PACK, CIN], BF16, name="w_raw%d" % k)
+            for h in range(2):
+                w_raw[(k, h)] = whole[:, :, h * HALF : (h + 1) * HALF]
+            w_raw[k] = whole[:]
         for h in range(2):
             for k in range(NDIR):
-                w_raw[(k, h)] = keep.tile([P, PACK, HALF], BF16, name="w_raw%d_%d" % (k, h))
                 w_c[(k, h)] = keep.tile([P, WOFF + HALF], U32, name="w_c%d_%d" % (k, h), align_bytes=256)
                 w_s[(k, h)] = keep.tile([P, 4 * SLOT], U8, name="w_s%d_%d" % (k, h), align_bytes=256)
         w_grp = {}
@@ -90,10 +105,8 @@ def tile_stackeddirectionalconv3d_t_kernel(tc, x, W, grad_out, out):
         nc.vector.memset(dir_s[2][:].bitcast(I32), 0)
         nc.vector.memset(dir_s[3][:].bitcast(I32), 0)
 
-        def lw(k, h, c0, c1):
-            nc.sync.dma_start(
-                out=w_raw[(k, h)][:, :, c0:c1], in_=w_view[k][:, :, h * HALF + c0 : h * HALF + c1]
-            )
+        def lw(k, h):
+            nc.sync.dma_start(out=w_raw[(k, h)], in_=w_view[k][:, :, h * HALF : (h + 1) * HALF])
 
         def lg(b, v0, v1):
             nc.sync.dma_start(out=g_raw[:, b, :, v0:v1], in_=g_view[b][:, :, v0:v1])
@@ -140,7 +153,11 @@ def tile_stackeddirectionalconv3d_t_kernel(tc, x, W, grad_out, out):
                 w_grp[(k, h)] = stage.tile(
                     [P, HALF, PACK], BF16, tag="w_grp", name="w_grp%d_%d" % (k, h), align_bytes=64
                 )
-            regroup(on_vector, w_grp[(k, h)][:, c0:c1, :], w_raw[(k, h)][:, :, c0:c1])
+            if (k, h) == (0, 0):
+                src = w_first[c0 // 256][:, :, c0 % 256 : c0 % 256 + c1 - c0]
+            else:
+                src = w_raw[(k, h)][:, :, c0:c1]
+            regroup(on_vector, w_grp[(k, h)][:, c0:c1, :], src)
 
         def qw(k, h, c0, c1):
             nc.vector.quantize_mx(
@@ -170,15 +187,21 @@ def tile_stackeddirectionalconv3d_t_kernel(tc, x, W, grad_out, out):
                 stop=(k == NDIR - 1),
             )
 
-        def ev(m, b, on_vector):
-            res = outp.tile([P, VOX], F32, tag="res", name="res%d_%d" % (m, b))
-            if on_vector:
-                nc.vector.tensor_copy(out=res[:], in_=acc[(m, b)][:])
-            else:
-                nc.scalar.copy(out=res[:], in_=acc[(m, b)][:])
-            nc.sync.dma_start(out=o_view[b, m], in_=res[:])
+        res = {}
 
-        S_COLS = [0, 320, 192, 256, 320, 384, 384, 384, 0, 0, 0, 256, 256, 256]
+        def ev(m, b, on_vector):
+            if m not in res:
+                res[m] = outp.tile([P, NB, VOX], F32, tag="res", name="res%d" % m)
+            if on_vector:
+                nc.vector.tensor_copy(out=res[m][:, b, :], in_=acc[(m, b)][:])
+            else:
+                nc.scalar.copy(out=res[m][:, b, :], in_=acc[(m, b)][:])
+            if m == 7:
+                nc.sync.dma_start(out=o_view[m][:, b, :], in_=res[m][:, b, :])
+            elif b == 1:
+                nc.sync.dma_start(out=o_view[m], in_=res[m][:])
+
+        S_COLS = [0, 320, 256, 320, 320, 384, 384, 384, 0, 0, 64, 320, 384, 320]
 
         def rw_split(n):
             k, h = n % NDIR, n // NDIR
@@ -195,10 +218,15 @@ def tile_stackeddirectionalconv3d_t_kernel(tc, x, W, grad_out, out):
                 qc(k - 5)
 
         lg(0, 0, 512)
-        lw(0, 0, 0, 512)
+        nc.sync.dma_start(out=w_first[0], in_=w_view[0][:, :, 0:256])
         lg(1, 0, 512)
-        for n in range(1, 2 * NDIR):
-            lw(n % NDIR, n // NDIR, 0, 512)
+        nc.sync.dma_start(out=w_first[1], in_=w_view[0][:, :, 256:512])
+        for k in range(1, WHOLE):
+            lw(k, 0)
+        for k in range(WHOLE, NDIR):
+            nc.sync.dma_start(out=w_raw[k], in_=w_view[k])
+        for k in range(WHOLE):
+            lw(k, 1)
         warm = psum.tile([P, VOX], F32, tag="bank7", name="warm")
         for i in range(7):
             nc.tensor.matmul(warm[:], lhsT=zeros[:, 0:P], rhs=zeros[:], start=True, stop=True)
@@ -209,24 +237,24 @@ def tile_stackeddirectionalconv3d_t_kernel(tc, x, W, grad_out, out):
         qg(0, 0, 512)
         rw(0, 0, 0, 128, False)
         rw(0, 0, 128, 256, False)
-        rw(0, 0, 256, 384, True)
         qw(0, 0, 0, 128)
-        qw(0, 0, 256, 384)
         rg(1, 320, 512, False)
         rg(1, 0, 320, True)
         qw(0, 0, 128, 256)
         qg(1, 0, 512)
-        rw(0, 0, 384, 512, False)
+        rw(0, 0, 256, 384, False)
+        rw(0, 0, 384, 512, True)
+        qw(0, 0, 256, 384)
         qw(0, 0, 384, 512)
         rw(1, 0, 0, 128, False)
         rw(1, 0, 128, 384, True)
         rw(1, 0, 384, 512, False)
-        for m in (0, 2, 1):
-            mx(0, m, 0, 2 * m)
-        for m in (0, 2, 1):
-            mx(0, m, 1, 2 * m + 1)
         for b in range(2):
-            mx(0, 3, b, 6 + b)
+            for m in (0, 1):
+                mx(0, m, b, 2 * m + b)
+        for m in (2, 3):
+            for b in range(2):
+                mx(0, m, b, 2 * m + b)
         for k in range(1, NDIR):
             prep(k)
             if k == 1:

@@ -238,10 +238,11 @@ def tile_stackeddirectionalconv3d_t_kernel(tc, x, W, grad_out, out):
         rw(0, 0, 0, 128, False)
         rw(0, 0, 128, 256, False)
         qw(0, 0, 0, 128)
-        rg(1, 320, 512, False)
-        rg(1, 0, 320, True)
+        rg(1, 256, 512, False)
+        rg(1, 0, 256, True)
         qw(0, 0, 128, 256)
-        qg(1, 0, 512)
+        qg(1, 0, 256)
+        qg(1, 256, 512)
         rw(0, 0, 256, 384, False)
         rw(0, 0, 384, 512, True)
         qw(0, 0, 256, 384)

from contextlib import ExitStack

import concourse.mybir as mybir

F32 = mybir.dt.float32
BF16 = mybir.dt.bfloat16
U32 = mybir.dt.uint32
I32 = mybir.dt.int32
U8 = mybir.dt.uint8
E4M3X4 = mybir.dt.float8_e4m3fn_x4
E5M2X4 = mybir.dt.float8_e5m2_x4

P = 128
PACK = 4
NB = 2
CIN = 1024
COUT = 512
VOX = 512
NDIR = 7
HALF = 512
PAD = 64
SLOT = 128
WOFF = 48
WHOLE = 5

FLOPS = 2 * NB * VOX * COUT * NDIR * CIN
BYTES = NDIR * COUT * CIN * 2 + NB * COUT * VOX * 2 + NB * CIN * VOX * 4

MANUAL = True


def tile_stackeddirectionalconv3d_t_kernel(tc, x, W, grad_out, out):
    nc = tc.nc
    w_view = W.rearrange("(k p j) i -> k p j i", k=NDIR, j=PACK)
    g_view = grad_out.rearrange("b (p j) t r c -> b p j (t r c)", j=PACK)
    o_view = out.rearrange("b (m p) t r c -> m p b (t r c)", p=P)

    with ExitStack() as ctx:
        keep = ctx.enter_context(tc.tile_pool(name="keep", bufs=1))
        stage = ctx.enter_context(tc.tile_pool(name="stage", bufs=4))
        outp = ctx.enter_context(tc.tile_pool(name="outp", bufs=8))
        psum = ctx.enter_context(tc.psum_pool(name="psum", bufs=1))
        if MANUAL:
            ctx.enter_context(tc.manual_schedule())

        g_raw = keep.tile([P, NB, PACK, VOX], BF16, name="g_raw")
        g_grp = keep.tile([P, NB, VOX, PACK], BF16, name="g_grp", align_bytes=64)
        base_c = keep.tile([P, NB, VOX + 2 * PAD], U32, name="base_c", align_bytes=256)
        base_s = keep.tile([P, NB, VOX + 2 * PAD], U8, name="base_s", align_bytes=256)
        dir_c = [
            keep.tile([P, NB, VOX], U32, name="dir_c%d" % d, align_bytes=256)
            for d in range(4)
        ]
        dir_s = [
            keep.tile([P, NB, VOX], U8, name="dir_s%d" % d, align_bytes=256)
            for d in range(4)
        ]
        w_raw = {}
        w_first = []
        for i in range(2):
            piece = keep.tile([P, PACK, HALF // 2], BF16, name="w_first%d" % i)
            w_first.append(piece[:])
        w_c = {}
        w_s = {}
        for k in range(WHOLE):
            for h in range(2):
                if (k, h) == (0, 0):
                    continue
                half = keep.tile([P, PACK, HALF], BF16, name="w_raw%d_%d" % (k, h))
                w_raw[(k, h)] = half[:]
        for k in range(WHOLE, NDIR):
            whole = keep.tile([P, PACK, CIN], BF16, name="w_raw%d" % k)
            for h in range(2):
                w_raw[(k, h)] = whole[:, :, h * HALF : (h + 1) * HALF]
            w_raw[k] = whole[:]
        for h in range(2):
            for k in range(NDIR):
                w_c[(k, h)] = keep.tile([P, WOFF + HALF], U32, name="w_c%d_%d" % (k, h), align_bytes=256)
                w_s[(k, h)] = keep.tile([P, 4 * SLOT], U8, name="w_s%d_%d" % (k, h), align_bytes=256)
        w_grp = {}
        acc = {}
        zeros = keep.tile([P, VOX], BF16, name="zeros")
        nc.vector.memset(zeros[:], 0.0)

        base_c32 = base_c[:].bitcast(I32)
        base_s32 = base_s[:].bitcast(I32)
        data_c32 = base_c32[:, :, PAD : PAD + VOX].rearrange("p b (t q) -> p b t q", q=64)
        data_s32 = base_s32[:, :, PAD // 4 : (PAD + VOX) // 4].rearrange("p b (t q) -> p b t q", q=16)
        dir_c32 = [dir_c[d][:].bitcast(I32).rearrange("p b (t q) -> p b t q", q=64) for d in range(2)]
        dir_s32 = [dir_s[d][:].bitcast(I32).rearrange("p b (t q) -> p b t q", q=16) for d in range(2)]
        row_c32 = base_c32[:, :, PAD : PAD + VOX].rearrange("p b (a c) -> p b a c", c=8)
        row_s8 = base_s[:, :, PAD : PAD + VOX].rearrange("p b (a c) -> p b a c", c=8)
        col_c32 = [dir_c[2 + d][:].bitcast(I32).rearrange("p b (a c) -> p b a c", c=8) for d in range(2)]
        col_s8 = [dir_s[2 + d][:].rearrange("p b (a c) -> p b a c", c=8) for d in range(2)]

        nc.vector.memset(base_s32, 0)
        nc.vector.memset(base_c32[:, :, 0:PAD], 0)
        nc.vector.memset(base_c32[:, :, PAD + VOX : PAD + VOX + PAD], 0)
        nc.vector.memset(dir_c32[0][:, :, :, 56:64], 0)
        nc.vector.memset(dir_c32[1][:, :, :, 0:8], 0)
        nc.vector.memset(dir_s32[0][:, :, :, 14:16], 0)
        nc.vector.memset(dir_s32[1][:, :, :, 0:2], 0)
        nc.vector.memset(col_c32[0][:, :, :, 7:8], 0)
        nc.vector.memset(col_c32[1][:, :, :, 0:1], 0)
        nc.vector.memset(dir_s[2][:].bitcast(I32), 0)
        nc.vector.memset(dir_s[3][:].bitcast(I32), 0)

        def lw(k, h):
            nc.sync.dma_start(out=w_raw[(k, h)], in_=w_view[k][:, :, h * HALF : (h + 1) * HALF])

        def lg(b, v0, v1):
            nc.sync.dma_start(out=g_raw[:, b, :, v0:v1], in_=g_view[b][:, :, v0:v1])

        def regroup(on_vector, dst, src):
            copy = nc.vector.tensor_copy if on_vector else nc.scalar.copy
            copy(
                out=dst.rearrange("p (c i) t -> p c t i", i=4),
                in_=src.rearrange("p t (c i) -> p c t i", i=4),
            )

        def rg(b, v0, v1, on_vector):
            regroup(on_vector, g_grp[:, b, v0:v1, :], g_raw[:, b, :, v0:v1])

        def qg(b, v0, v1):
            nc.vector.quantize_mx(
                out=base_c[:, b, PAD + v0 : PAD + v1].bitcast(E5M2X4),
                scales=base_s[:, b, PAD + v0 : PAD + v1],
                in_=g_grp[:, b, v0:v1, :].rearrange("p w j -> p (w j)"),
            )

        def mr(d):
            if d == 0:
                nc.vector.tensor_copy(out=dir_c32[0][:, :, :, 0:56], in_=data_c32[:, :, :, 8:64])
                nc.vector.tensor_copy(out=dir_s32[0][:, :, :, 0:14], in_=data_s32[:, :, :, 2:16])
            else:
                nc.vector.tensor_copy(out=dir_c32[1][:, :, :, 8:64], in_=data_c32[:, :, :, 0:56])
                nc.vector.tensor_copy(out=dir_s32[1][:, :, :, 2:16], in_=data_s32[:, :, :, 0:14])

        def sc(d):
            if d == 0:
                nc.vector.tensor_copy(out=col_c32[0][:, :, :, 0:7], in_=row_c32[:, :, :, 1:8])
            else:
                nc.vector.tensor_copy(out=col_c32[1][:, :, :, 1:8], in_=row_c32[:, :, :, 0:7])

        def qc(d):
            if d == 0:
                nc.vector.tensor_copy(out=col_s8[0][:, :, :, 0:7], in_=row_s8[:, :, :, 1:8])
            else:
                nc.vector.tensor_copy(out=col_s8[1][:, :, :, 1:8], in_=row_s8[:, :, :, 0:7])

        def rw(k, h, c0, c1, on_vector):
            if (k, h) not in w_grp:
                w_grp[(k, h)] = stage.tile(
                    [P, HALF, PACK], BF16, tag="w_grp", name="w_grp%d_%d" % (k, h), align_bytes=64
                )
            if (k, h) == (0, 0):
                src = w_first[c0 // 256][:, :, c0 % 256 : c0 % 256 + c1 - c0]
            else:
                src = w_raw[(k, h)][:, :, c0:c1]
            regroup(on_vector, w_grp[(k, h)][:, c0:c1, :], src)

        def qw(k, h, c0, c1):
            nc.vector.quantize_mx(
                out=w_c[(k, h)][:, WOFF + c0 : WOFF + c1].bitcast(E4M3X4),
                scales=w_s[(k, h)][:, c0:c1],
                in_=w_grp[(k, h)][:, c0:c1, :].rearrange("p w j -> p (w j)"),
            )

        def moving(k, b):
            if k < 3:
                v0 = (PAD, 2 * PAD, 0)[k]
                return base_c[:, b, v0 : v0 + VOX], base_s[:, b, v0 : v0 + VOX]
            return dir_c[k - 3][:, b, :], dir_s[k - 3][:, b, :]

        def mx(k, m, b, bank):
            if k == 0:
                acc[(m, b)] = psum.tile([P, VOX], F32, tag="bank%d" % bank, name="acc%d_%d" % (m, b))
            h = m // 4
            codes, scales = moving(k, b)
            nc.tensor.matmul_mx(
                out=acc[(m, b)][:],
                lhsT=w_c[(k, h)][:, WOFF + (m % 4) * P : WOFF + (m % 4 + 1) * P].bitcast(E4M3X4),
                lhsT_scale=w_s[(k, h)][:, (m % 4) * SLOT : (m % 4) * SLOT + P],
                rhs=codes.bitcast(E5M2X4),
                rhs_scale=scales,
                start=(k == 0),
                stop=(k == NDIR - 1),
            )

        res = {}

        def ev(m, b, on_vector):
            if m not in res:
                res[m] = outp.tile([P, NB, VOX], F32, tag="res", name="res%d" % m)
            if on_vector:
                nc.vector.tensor_copy(out=res[m][:, b, :], in_=acc[(m, b)][:])
            else:
                nc.scalar.copy(out=res[m][:, b, :], in_=acc[(m, b)][:])
            if m == 7:
                nc.sync.dma_start(out=o_view[m][:, b, :], in_=res[m][:, b, :])
            elif b == 1:
                nc.sync.dma_start(out=o_view[m], in_=res[m][:])

        S_COLS = [0, 320, 256, 320, 320, 384, 384, 384, 0, 0, 64, 320, 384, 320]

        def rw_split(n):
            k, h = n % NDIR, n // NDIR
            if S_COLS[n] > 0:
                rw(k, h, 0, S_COLS[n], False)
            if S_COLS[n] < HALF:
                rw(k, h, S_COLS[n], HALF, True)

        def prep(k):
            if k == 3 or k == 4:
                mr(k - 3)
            elif k == 5 or k == 6:
                sc(k - 5)
                qc(k - 5)

        lg(0, 0, 512)
        nc.sync.dma_start(out=w_first[0], in_=w_view[0][:, :, 0:256])
        lg(1, 0, 512)
        nc.sync.dma_start(out=w_first[1], in_=w_view[0][:, :, 256:512])
        for k in range(1, WHOLE):
            lw(k, 0)
        for k in range(WHOLE, NDIR):
            nc.sync.dma_start(out=w_raw[k], in_=w_view[k])
        for k in range(WHOLE):
            lw(k, 1)
        warm = psum.tile([P, VOX], F32, tag="bank7", name="warm")
        for i in range(7):
            nc.tensor.matmul(warm[:], lhsT=zeros[:, 0:P], rhs=zeros[:], start=True, stop=True)
        for i in range(5):
            nc.tensor.matmul(warm[:], lhsT=zeros[:, 0:P], rhs=g_raw[:, 0, i % PACK, :], start=True, stop=True)
        rg(0, 0, 320, True)
        rg(0, 320, 512, False)
        qg(0, 0, 512)
        rw(0, 0, 0, 128, False)
        rw(0, 0, 128, 256, False)
        qw(0, 0, 0, 128)
        rg(1, 256, 512, False)
        rg(1, 0, 256, True)
        qw(0, 0, 128, 256)
        qg(1, 0, 256)
        qg(1, 256, 512)
        rw(0, 0, 256, 384, False)
        rw(0, 0, 384, 512, True)
        qw(0, 0, 256, 384)
        qw(0, 0, 384, 512)
        rw(1, 0, 0, 128, False)
        rw(1, 0, 128, 384, True)
        rw(1, 0, 384, 512, False)
        for b in range(2):
            for m in (0, 1):
                mx(0, m, b, 2 * m + b)
        for m in (2, 3):
            for b in range(2):
                mx(0, m, b, 2 * m + b)
        for k in range(1, NDIR):
            prep(k)
            if k == 1:
                for c0 in range(0, HALF, P):
                    qw(k, 0, c0, c0 + P)
            else:
                qw(k, 0, 0, 512)
            rw_split(k + 1)
            for m in range(4):
                for b in range(NB):
                    mx(k, m, b, 2 * m + b)
        qw(0, 1, 0, 512)
        rw_split(NDIR + 1)
        qw(1, 1, 0, 512)
        rw_split(NDIR + 2)
        for m in range(2):
            for b in range(NB):
                ev(m, b, False)
        for k in range(2):
            for m in range(4, 6):
                for b in range(NB):
                    mx(k, m, b, 2 * (m - 4) + b)
        for b in range(NB):
            ev(2, b, False)
        for k in range(2):
            for b in range(NB):
                mx(k, 6, b, 4 + b)
        for b in range(NB):
            ev(3, b, False)
        for k in range(2, NDIR):
            qw(k, 1, 0, 512)
            if k + 1 < NDIR:
                rw_split(NDIR + k + 1)
            for m in range(4, 7):
                for b in range(NB):
                    mx(k, m, b, 2 * (m - 4) + b)
        for k in range(NDIR):
            mx(k, 7, 0, 6)
        for m in range(4, 7):
            ev(m, 0, False)
            ev(m, 1, True)
        ev(7, 0, True)
        for k in range(NDIR):
            mx(k, 7, 1, 7)
        ev(7, 1, False)
